import numpy as np
import ml_dtypes


def mxq(x, axis, fmt="e4m3"):
    dtype, down = {"e4m3": (ml_dtypes.float8_e4m3fn, 7), "e5m2": (ml_dtypes.float8_e5m2, 14)}[fmt]
    v = np.moveaxis(np.asarray(x, np.float32).astype(ml_dtypes.bfloat16).astype(np.float64), axis, -1)
    blocks = v.reshape(v.shape[:-1] + (-1, 32))
    amax = np.abs(blocks).max(-1, keepdims=True)
    byte = np.maximum(np.where(amax > 0, np.frexp(amax)[1] - 1 + 127, 0) - down, 1)
    scale = np.exp2(byte - 127.0)
    codes = (blocks / scale).astype(np.float32).astype(dtype).astype(np.float64)
    return np.moveaxis((codes * scale).reshape(v.shape), -1, axis)


WIDE = False


def mx_kscale(k):
    if not WIDE:
        return np.ones(k)
    levels = np.array([10, -10, 5, -5, 0])
    a = np.random.permutation(np.resize(levels, k // 512 * 4)).reshape(k // 512, 4)
    idx = np.arange(k)
    return np.exp2(a[idx // 512, idx % 128 // 32])


BF16 = ml_dtypes.bfloat16


def bf(x):
    return np.asarray(x, np.float32).astype(BF16)


def f64(x):
    return np.asarray(x).astype(np.float64)


N, C, T, R = 1, 1024, 1024, 16
G = 2.25


def mix(a, z):
    out = np.zeros((N, C, T))
    for r in range(R):
        out += a[:, :, r, None] * z[:, r, None, :]
    return out


def setup_inputs():
    s = mx_kscale(T)
    a = np.sqrt(G / np.sqrt(R))
    z = np.random.standard_normal((N, R, T))
    x = mix(a * np.random.standard_normal((N, C, R)), z) + np.random.standard_normal((N, C, T))
    m = mix(a * np.random.standard_normal((N, C, R)), z) + np.random.standard_normal((N, C, T))
    return {"feature_x": bf(x * s), "feature_m": bf(m / s)}


def reference(feature_x, feature_m):
    x, m = f64(feature_x), f64(feature_m)
    logits = (mxq(x, 2, "e4m3") @ mxq(m, 2, "e4m3").transpose(0, 2, 1)) / T
    e = np.exp(logits - logits.max(-1, keepdims=True))
    attn = e / e.sum(-1, keepdims=True)
    cross_x = (mxq(attn, 1, "e4m3").transpose(0, 2, 1) @ mxq(x, 1, "e4m3")) + x
    cross_m = (mxq(attn, 2, "e4m3") @ mxq(m, 1, "e4m3")) + m
    return cross_x, cross_m

@@ -1,0 +1,347 @@
+from contextlib import ExitStack
+
+import concourse.mybir as mybir
+from concourse.masks import make_identity
+
+FLOPS = 3 * 2 * 1024 * 1024 * 1024
+
+F32 = mybir.dt.float32
+BF16 = mybir.dt.bfloat16
+U32 = mybir.dt.uint32
+U8 = mybir.dt.uint8
+FP8X4 = mybir.dt.float8_e4m3fn_x4
+ALU = mybir.AluOpType
+ACT = mybir.ActivationFunctionType
+AX = mybir.AxisListType
+
+P = 128
+C = 1024
+T = 1024
+HALF = 512
+
+
+PS_BUFS = {"L": 3, "T": 2, "O": 3}
+CH_BUFS = 5
+NORM = "G"
+GSEL = 2
+AC11 = "V"
+HEAD_ENG = ("S", "V", "S", "V", "S", "V", "S", "V")
+HEAD_V = {}
+XT_AT = {-1: [(1, "L"), (2, "T"), (3, "T")], 0: [(4, "O"), (5, "O"), (6, "O")], 1: [(7, "T")]}
+S_FIRST = {-1: [("xc", "", 1, 0), ("xc", "", 2, 0), ("xc", "", 3, 0)]}
+V_FIRST = {-1: [("xq", "", 1, 0)]}
+V_EXTRA = {
+    0: [("xq", "", 2, 0), ("c", "mc", 0, 1), ("q", "mc", 0, 0), ("c", "mc", 1, 0)],
+    1: [("xq", "", 3, 0), ("q", "mc", 0, 1), ("c", "mc", 1, 1), ("q", "mc", 1, 0), ("xq", "", 4, 0), ("q", "mc", 1, 1)],
+    2: [("xq", "", 5, 0), ("xq", "", 6, 0)],
+    3: [("xq", "", 7, 0), ("q", "xc", 0, 0)],
+    4: [("q", "xc", 0, 1)],
+    5: [("c", "ac", 0, 0), ("q", "xc", 1, 0)],
+    6: [("q", "ac", 0, 0), ("q", "xc", 1, 1)],
+    7: [("q", "ac", 0, 1)],
+}
+S_EXTRA = {-1: [("c0", "mc", 0, 0), ("c1", "mc", 0, 0)],
+           0: [("xc", "", 4, 0), ("xc", "", 5, 0), ("xc", "", 6, 0)], 1: [("xc", "", 7, 0), ("c0", "xc", 0, 0)],
+           2: [("c1", "xc", 0, 0), ("c0", "xc", 0, 1)], 3: [("c1", "xc", 0, 1), ("c0", "xc", 1, 0)], 4: [("c1", "xc", 1, 0), ("c0", "xc", 1, 1)],
+           5: [("c1", "xc", 1, 1), ("c0", "ac", 0, 1)], 6: [("c1", "ac", 0, 1)]}
+
+
+def tile_crossxmfusion_pa_kernel(tc, feature_x, feature_m, out_0, out_1):
+    nc = tc.nc
+    xv = feature_x.flatten_outer_dims().rearrange("(g p j) t -> p g j t", g=2, j=4)
+    mv = feature_m.flatten_outer_dims().rearrange("(g p j) t -> p g j t", g=2, j=4)
+    o0v = out_0.flatten_outer_dims().rearrange("(g p j) t -> p g j t", g=2, j=4)
+    o1v = out_1.flatten_outer_dims().rearrange("(g p j) t -> p g j t", g=2, j=4)
+
+    with ExitStack() as ctx:
+        keep = ctx.enter_context(tc.tile_pool(name="keep", bufs=1))
+        stage = ctx.enter_context(tc.tile_pool(name="stage", bufs=2))
+        small = ctx.enter_context(tc.tile_pool(name="small", bufs=4))
+        psum = ctx.enter_context(tc.psum_pool(name="psum", bufs=2))
+        ctx.enter_context(tc.manual_schedule())
+
+        ident_f = keep.tile([P, P], F32, name="ident_f")
+        make_identity(nc, ident_f[:])
+        ident_b = keep.tile([P, P], BF16, name="ident_b")
+        make_identity(nc, ident_b[:])
+
+        x_sb = [keep.tile([P, 4, T], BF16, name="x_sb%d" % g, align_bytes=64) for g in range(2)]
+        m_sb = [keep.tile([P, 4, T], BF16, name="m_sb%d" % g, align_bytes=64) for g in range(2)]
+
+        def load(dst, src, g, h):
+            nc.sync.dma_start(out=dst[g][:, 2 * h : 2 * h + 2, :], in_=src[:, g, 2 * h : 2 * h + 2, :])
+
+        for g in range(2):
+            for h in range(2):
+                load(m_sb, mv, g, h)
+        nc.sync.dma_start(out=x_sb[0][:, 0:1, :], in_=xv[:, 0, 0:1, :])
+        nc.sync.dma_start(out=x_sb[0][:, 1:4, :], in_=xv[:, 0, 1:4, :])
+        load(x_sb, xv, 1, 0)
+        load(x_sb, xv, 1, 1)
+
+        def codes_and_scales(name):
+            return (
+                keep.tile([P, 2048], U32, name=name + "_codes", align_bytes=64),
+                keep.tile([P, 2048], U8, name=name + "_scales", align_bytes=64),
+            )
+
+        xt_codes, xt_scales = codes_and_scales("xt")
+        mt_codes, mt_scales = codes_and_scales("mt")
+        xc_codes, xc_scales = codes_and_scales("xc")
+        mc_codes, mc_scales = codes_and_scales("mc")
+        ac_codes, ac_scales = codes_and_scales("ac")
+        at_codes, at_scales = codes_and_scales("at")
+
+        def quantise(codes, scales, start, grouped):
+            words = grouped.shape[1] // 4
+            nc.vector.quantize_mx(
+                out=codes[:, start : start + words].bitcast(FP8X4),
+                scales=scales[:, start : start + words],
+                in_=grouped,
+            )
+
+        def mx(out, a, a_start, b, b_start, start, stop):
+            nc.tensor.matmul_mx(
+                out=out,
+                lhsT=a[0][:, a_start : a_start + P].bitcast(FP8X4),
+                lhsT_scale=a[1][:, a_start : a_start + P],
+                rhs=b[0][:, b_start : b_start + HALF].bitcast(FP8X4),
+                rhs_scale=b[1][:, b_start : b_start + HALF],
+                start=start,
+                stop=stop,
+            )
+
+        def copy_on(engine, out, in_):
+            if engine == "S":
+                nc.scalar.copy(out=out, in_=in_)
+            else:
+                nc.vector.tensor_copy(out=out, in_=in_)
+
+        def bank(tag, shape, dtype):
+            return psum.tile(shape, dtype, name="ps" + tag, tag=tag, bufs=PS_BUFS[tag])
+
+        def transpose_words(row, tag):
+            words = row.bitcast(F32)
+            tw = bank(tag, [P, 4, P], F32)
+            for b in range(4):
+                nc.tensor.transpose(tw[:, b, :], words[:, P * b : P * (b + 1)], ident_f[:])
+            return tw[:].rearrange("p (s u) c -> p s c u", s=2, u=2)
+
+        st = {}
+
+        def xt_transpose(i, tag):
+            st["xtp", i] = transpose_words(x_sb[i // 4][:, i % 4, :], tag)
+
+        def xt_copy(i, engine):
+            xt_g = stage.tile([P, 1024], BF16, name="xt_g", bufs=6, align_bytes=64)
+            copy_on(engine, xt_g[:].bitcast(F32).rearrange("p (s c u) -> p s c u", s=2, u=2), st["xtp", i])
+            st["xtg", i] = xt_g
+
+        def xt_quant(i):
+            quantise(xt_codes, xt_scales, i * 256, st["xtg", i][:])
+
+        def mt_transpose(i, tag):
+            st["mtp", i] = transpose_words(m_sb[i // 4][:, i % 4, :], tag)
+
+        def mt_copy(i, engine):
+            g, j = divmod(i, 4)
+            if j == 0:
+                st["mtg", g] = stage.tile([P, 4096], BF16, name="mt_g", bufs=2, align_bytes=64)
+            view = st["mtg", g][:].bitcast(F32).rearrange("p (s n u) -> p s n u", s=2, u=2)
+            copy_on(engine, view[:, :, P * j : P * (j + 1), :], st["mtp", i])
+
+        def mt_quant(g, s, pair):
+            quantise(mt_codes, mt_scales, s * 1024 + g * HALF + pair * 256,
+                     st["mtg", g][:, s * 2048 + pair * 1024 : s * 2048 + (pair + 1) * 1024])
+
+        def ch_copy(key, src, g, half, engine, lo=0, hi=HALF):
+            if lo == 0:
+                st[key, g, half] = stage.tile([P, HALF, 4], BF16, name="ch_g", bufs=CH_BUFS, align_bytes=64)
+            copy_on(engine, st[key, g, half][:, lo:hi, :].rearrange("p (c i) j -> p c j i", i=4),
+                    src[g][:, :, half * HALF + lo : half * HALF + hi].rearrange("p j (c i) -> p c j i", i=4))
+
+        def ch_quant(key, pair, g, half):
+            quantise(pair[0], pair[1], g * 1024 + half * HALF, st[key, g, half][:].rearrange("p c j -> p (c j)"))
+
+        attn_bf = [keep.tile([P, 4, C], BF16, name="attn_bf%d" % g, align_bytes=64) for g in range(2)]
+
+        def logits(i):
+            st["lg", i] = [bank("L", [P, HALF], F32) for h in range(2)]
+            for h in range(2):
+                for s in range(2):
+                    mx(st["lg", i][h][:], (xt_codes, xt_scales), i * 256 + s * P,
+                       (mt_codes, mt_scales), s * 1024 + h * HALF, s == 0, s == 1)
+
+        def row_max(i):
+            mx2 = small.tile([P, 2], F32, name="mx2")
+            for h in range(2):
+                nc.vector.tensor_reduce(out=mx2[:, h : h + 1], in_=st["lg", i][h][:], axis=AX.X, op=ALU.max)
+            nb = small.tile([P, 1], F32, name="nb")
+            nc.vector.tensor_scalar(out=nb[:], in0=mx2[:, 0:1], scalar1=mx2[:, 1:2], scalar2=-1.0 / T,
+                                    op0=ALU.max, op1=ALU.mult)
+            st["nb", i] = nb
+
+        def exps(i):
+            e = stage.tile([P, C], F32, name="e", bufs=3)
+            s2 = small.tile([P, 2], F32, name="s2")
+            for h in range(2):
+                nc.scalar.activation(out=e[:, h * HALF : (h + 1) * HALF], in_=st["lg", i][h][:], func=ACT.Exp,
+                                     bias=st["nb", i][:], scale=1.0 / T, accum_out=s2[:, h : h + 1])
+            st["e", i] = e
+            st["s2", i] = s2
+
+        def row_recip(i):
+            s2 = st["s2", i]
+            ssum = small.tile([P, 1], F32, name="ssum")
+            nc.vector.tensor_scalar(out=ssum[:], in0=s2[:, 0:1], scalar1=s2[:, 1:2], scalar2=None, op0=ALU.add)
+            r = small.tile([P, 1], F32, name="r")
+            nc.vector.reciprocal(out=r[:], in_=ssum[:])
+            st["r", i] = r
+
+        def normalise(i, engine):
+            out = attn_bf[i // 4][:, i % 4, :]
+            if engine == "S":
+                nc.scalar.activation(out=out, in_=st["e", i][:], func=ACT.Copy, scale=st["r", i][:])
+            elif engine == "V":
+                nc.vector.tensor_scalar(out=out, in0=st["e", i][:], scalar1=st["r", i][:], scalar2=None, op0=ALU.mult)
+            else:
+                nc.gpsimd.tensor_scalar(out=out, in0=st["e", i][:], scalar1=st["r", i][:], scalar2=0.0,
+                                        op0=ALU.mult, op1=ALU.add)
+
+        def at_transpose(i):
+            at_ps = bank("T", [P, 8, P], BF16)
+            for b in range(8):
+                nc.tensor.transpose(at_ps[:, b, :], attn_bf[i // 4][:, i % 4, P * b : P * (b + 1)], ident_b[:])
+            st["atp", i] = at_ps
+
+        def at_copy(i, engine):
+            at_g = stage.tile([P, 1024], BF16, name="at_g", bufs=3, align_bytes=64)
+            copy_on(engine, at_g[:].rearrange("p (s c k) -> p s c k", s=2, k=4),
+                    st["atp", i][:].rearrange("p (s k) c -> p s c k", s=2, k=4))
+            st["atg", i] = at_g
+
+        def at_quant(i):
+            quantise(at_codes, at_scales, i * 256, st["atg", i][:])
+
+        def product(key, i, h, tag, passes=(0, 1)):
+            if passes[0] == 0:
+                st["acc", key, i, h] = bank(tag, [P, HALF], F32)
+            acc = st["acc", key, i, h]
+            for s in passes:
+                if key == "m":
+                    mx(acc[:], (at_codes, at_scales), i * 256 + s * P, (mc_codes, mc_scales), s * 1024 + h * HALF, s == 0, s == 1)
+                else:
+                    mx(acc[:], (ac_codes, ac_scales), s * 1024 + i * P, (xc_codes, xc_scales), s * 1024 + h * HALF, s == 0, s == 1)
+
+        def residual(key, i, h, engine="V"):
+            g, j = divmod(i, 4)
+            if h == 0:
+                st["res", key, i] = stage.tile([P, T], F32, name="res", bufs=6)
+            res = st["res", key, i]
+            src = (m_sb if key == "m" else x_sb)[g]
+            cols = slice(h * HALF, (h + 1) * HALF)
+            if engine == "V":
+                nc.vector.tensor_tensor(out=res[:, cols], in0=st["acc", key, i, h][:], in1=src[:, j, cols], op=ALU.add)
+            else:
+                nc.scalar.copy(out=res[:, cols], in_=st["acc", key, i, h][:])
+                nc.gpsimd.tensor_tensor(out=res[:, cols], in0=res[:, cols], in1=src[:, j, cols], op=ALU.add)
+
+        def store(key, i, lo=0, hi=T):
+            g, j = divmod(i, 4)
+            nc.sync.dma_start(out=(o1v if key == "m" else o0v)[:, g, j, lo:hi], in_=st["res", key, i][:, lo:hi])
+
+        SRC = {"mc": m_sb, "xc": x_sb, "ac": attn_bf}
+        DST = {"mc": (mc_codes, mc_scales), "xc": (xc_codes, xc_scales), "ac": (ac_codes, ac_scales)}
+
+        def extras(items, engine):
+            for kind, key, g, half in items:
+                if kind == "c":
+                    ch_copy(key, SRC[key], g, half, engine)
+                elif kind == "c0":
+                    ch_copy(key, SRC[key], g, half, engine, 0, 256)
+                elif kind == "c1":
+                    ch_copy(key, SRC[key], g, half, engine, 256, 512)
+                elif kind == "q":
+                    ch_quant(key, DST[key], g, half)
+                elif kind == "xc":
+                    xt_copy(g, engine)
+                else:
+                    xt_quant(g)
+
+        head_tags = ("L", "L", "L", "O", "O", "O", "T", "T")
+        for i in range(8):
+            mt_transpose(i, head_tags[i])
+            mt_copy(i, HEAD_ENG[i])
+            if i % 2 == 1:
+                mt_quant(i // 4, 0, (i % 4) // 2)
+                mt_quant(i // 4, 1, (i % 4) // 2)
+            extras(HEAD_V.get(i, []), "V")
+        xt_transpose(0, "L")
+        xt_copy(0, "S")
+        xt_quant(0)
+
+        for k in range(-1, 8):
+            if 0 <= k:
+                exps(k)
+            if 0 <= k - 1:
+                at_transpose(k - 1)
+            for i, tag in XT_AT.get(k, []):
+                xt_transpose(i, tag)
+            if 0 <= k - 2:
+                at_quant(k - 2)
+                product("m", k - 2, 0, "O")
+                product("m", k - 2, 1, "O")
+            extras(S_FIRST.get(k, []), "S")
+            extras(V_FIRST.get(k, []), "V")
+            if k + 1 < 8:
+                logits(k + 1)
+            if 0 <= k - 1:
+                at_copy(k - 1, "S")
+            if k >= 0:
+                extras(V_EXTRA.get(k, []), "V")
+                row_recip(k)
+                normalise(k, NORM)
+            if 0 <= k - 2:
+                residual("m", k - 2, 0)
+                residual("m", k - 2, 1)
+                store("m", k - 2)
+            if k == 7:
+                at_quant(6)
+            if k + 1 < 8:
+                row_max(k + 1)
+            extras(S_EXTRA.get(k, []), "S")
+
+        product("m", 6, 0, "O")
+        product("m", 6, 1, "O")
+        at_transpose(7)
+        early = (("L", 0, 0), ("L", 0, 1), ("L", 1, 0), ("T", 1, 1))
+        for tag, b, h in early:
+            product("x", b, h, tag, (0,))
+        at_copy(7, "S")
+        ch_copy("ac", attn_bf, 1, 0, "V")
+        residual("m", 6, 0)
+        ch_quant("ac", DST["ac"], 1, 0)
+        ch_copy("ac", attn_bf, 1, 1, AC11)
+        residual("m", 6, 1)
+        store("m", 6)
+        at_quant(7)
+        for tag, b, h in early:
+            product("x", b, h, tag, (1,))
+        product("m", 7, 0, "O")
+        product("m", 7, 1, "O")
+        product("x", 2, 0, "T")
+        product("x", 2, 1, "O")
+        order = [("x", 0), ("x", 1), ("m", 7)] + [("x", b) for b in range(2, 8)]
+        later_tags = (("L", "L"), ("L", "T"), ("O", "O"), ("T", "O"), ("L", "L"))
+        for pos, (key, i) in enumerate(order):
+            for h in range(2):
+                residual(key, i, h, "G" if (2 * pos + h) % 3 == GSEL and pos >= 1 else "V")
+                if pos == len(order) - 1:
+                    store(key, i, h * HALF, (h + 1) * HALF)
+            if pos < len(order) - 1:
+                store(key, i)
+            if pos == 0:
+                ch_quant("ac", DST["ac"], 1, 1)
+            if pos + 4 < len(order):
+                for h in range(2):
+                    product("x", order[pos + 4][1], h, later_tags[pos][h])

@@ -20,30 +20,27 @@ T = 1024
 HALF = 512
 
 
-PS_BUFS = {"L": 3, "T": 2, "O": 3}
 CH_BUFS = 5
 NORM = "G"
 GSEL = 2
-AC11 = "V"
+AC_SPLIT = 336
+V_HEAD = []
 HEAD_ENG = ("S", "V", "S", "V", "S", "V", "S", "V")
-HEAD_V = {}
-XT_AT = {-1: [(1, "L"), (2, "T"), (3, "T")], 0: [(4, "O"), (5, "O"), (6, "O")], 1: [(7, "T")]}
-S_FIRST = {-1: [("xc", "", 1, 0), ("xc", "", 2, 0), ("xc", "", 3, 0)]}
-V_FIRST = {-1: [("xq", "", 1, 0)]}
+XT_AT = {0: [4, 5], 1: [6, 7]}
+V_FIRST = {0: [("xq", "", 2, 0)], 1: [("xq", "", 3, 0)], 2: [("xq", "", 4, 0)], 3: [("xq", "", 5, 0)], 4: [("xq", "", 6, 0)], 5: [("xq", "", 7, 0)]}
 V_EXTRA = {
-    0: [("xq", "", 2, 0), ("c", "mc", 0, 1), ("q", "mc", 0, 0), ("c", "mc", 1, 0)],
-    1: [("xq", "", 3, 0), ("q", "mc", 0, 1), ("c", "mc", 1, 1), ("q", "mc", 1, 0), ("xq", "", 4, 0), ("q", "mc", 1, 1)],
-    2: [("xq", "", 5, 0), ("xq", "", 6, 0)],
-    3: [("xq", "", 7, 0), ("q", "xc", 0, 0)],
-    4: [("q", "xc", 0, 1)],
-    5: [("c", "ac", 0, 0), ("q", "xc", 1, 0)],
-    6: [("q", "ac", 0, 0), ("q", "xc", 1, 1)],
-    7: [("q", "ac", 0, 1)],
+    0: [("c", "mc", 0, 1), ("c", "mc", 1, 0), ("q", "mc", 0, 1)],
+    1: [("q", "mc", 0, 0), ("c", "mc", 1, 1), ("q", "mc", 1, 0), ("q", "mc", 1, 1)],
+    2: [("c", "xc", 1, 1)],
+    3: [("q", "xc", 0, 0), ("q", "xc", 1, 1)],
+    4: [("c", "ac", 0, 0)],
+    5: [("q", "xc", 0, 1), ("q", "ac", 0, 0)],
+    6: [("c", "ac", 0, 1)],
+    7: [("q", "ac", 0, 1), ("q", "xc", 1, 0)],
 }
-S_EXTRA = {-1: [("c0", "mc", 0, 0), ("c1", "mc", 0, 0)],
-           0: [("xc", "", 4, 0), ("xc", "", 5, 0), ("xc", "", 6, 0)], 1: [("xc", "", 7, 0), ("c0", "xc", 0, 0)],
-           2: [("c1", "xc", 0, 0), ("c0", "xc", 0, 1)], 3: [("c1", "xc", 0, 1), ("c0", "xc", 1, 0)], 4: [("c1", "xc", 1, 0), ("c0", "xc", 1, 1)],
-           5: [("c1", "xc", 1, 1), ("c0", "ac", 0, 1)], 6: [("c1", "ac", 0, 1)]}
+S_EXTRA = {0: [("c0", "mc", 0, 0), ("c1", "mc", 0, 0), ("xc", "", 4, 0), ("xc", "", 5, 0)], 1: [("xc", "", 6, 0), ("xc", "", 7, 0), ("c0", "xc", 0, 0)],
+           2: [("c1", "xc", 0, 0)], 3: [("c0", "xc", 0, 1)], 4: [("c1", "xc", 0, 1)],
+           5: [("c0", "xc", 1, 0)], 6: [("c1", "xc", 1, 0)]}
 
 
 def tile_crossxmfusion_pa_kernel(tc, feature_x, feature_m, out_0, out_1):
@@ -59,6 +56,10 @@ def tile_crossxmfusion_pa_kernel(tc, feature_x, feature_m, out_0, out_1):
         small = ctx.enter_context(tc.tile_pool(name="small", bufs=4))
         psum = ctx.enter_context(tc.psum_pool(name="psum", bufs=2))
         ctx.enter_context(tc.manual_schedule())
+
+        warm = small.tile([P, 2], F32, name="warm")
+        nc.vector.memset(warm[:, 0:1], 0.0)
+        nc.scalar.activation(out=warm[:, 1:2], in_=warm[:, 0:1], func=ACT.Exp)
 
         ident_f = keep.tile([P, P], F32, name="ident_f")
         make_identity(nc, ident_f[:])
@@ -118,7 +119,7 @@ def tile_crossxmfusion_pa_kernel(tc, feature_x, feature_m, out_0, out_1):
                 nc.vector.tensor_copy(out=out, in_=in_)
 
         def bank(tag, shape, dtype):
-            return psum.tile(shape, dtype, name="ps" + tag, tag=tag, bufs=PS_BUFS[tag])
+            return psum.tile(shape, dtype, name="ps" + tag, tag="bank", bufs=8)
 
         def transpose_words(row, tag):
             words = row.bitcast(F32)
@@ -268,80 +269,80 @@ def tile_crossxmfusion_pa_kernel(tc, feature_x, feature_m, out_0, out_1):
                 else:
                     xt_quant(g)
 
-        head_tags = ("L", "L", "L", "O", "O", "O", "T", "T")
         for i in range(8):
-            mt_transpose(i, head_tags[i])
+            mt_transpose(i, "T")
             mt_copy(i, HEAD_ENG[i])
             if i % 2 == 1:
                 mt_quant(i // 4, 0, (i % 4) // 2)
                 mt_quant(i // 4, 1, (i % 4) // 2)
-            extras(HEAD_V.get(i, []), "V")
-        xt_transpose(0, "L")
-        xt_copy(0, "S")
-        xt_quant(0)
+        for i in range(4):
+            xt_transpose(i, "T")
+            xt_copy(i, "S")
+            if i < 2:
+                xt_quant(i)
+        logits(0)
+        logits(1)
+        extras(V_HEAD, "V")
+        row_max(0)
+        exps(0)
 
-        for k in range(-1, 8):
-            if 0 <= k:
-                exps(k)
+        for k in range(0, 8):
             if 0 <= k - 1:
                 at_transpose(k - 1)
-            for i, tag in XT_AT.get(k, []):
-                xt_transpose(i, tag)
+            for i in XT_AT.get(k, []):
+                xt_transpose(i, "T")
             if 0 <= k - 2:
                 at_quant(k - 2)
                 product("m", k - 2, 0, "O")
                 product("m", k - 2, 1, "O")
-            extras(S_FIRST.get(k, []), "S")
             extras(V_FIRST.get(k, []), "V")
-            if k + 1 < 8:
-                logits(k + 1)
+            if k + 2 < 8:
+                logits(k + 2)
             if 0 <= k - 1:
                 at_copy(k - 1, "S")
-            if k >= 0:
-                extras(V_EXTRA.get(k, []), "V")
-                row_recip(k)
-                normalise(k, NORM)
+            extras(V_EXTRA.get(k, []), "V")
+            extras(S_EXTRA.get(k, []), "S")
+            row_recip(k)
+            normalise(k, NORM)
+            if k + 1 < 8:
+                row_max(k + 1)
+                exps(k + 1)
             if 0 <= k - 2:
                 residual("m", k - 2, 0)
                 residual("m", k - 2, 1)
                 store("m", k - 2)
-            if k == 7:
-                at_quant(6)
-            if k + 1 < 8:
-                row_max(k + 1)
-            extras(S_EXTRA.get(k, []), "S")
 
+        at_quant(6)
         product("m", 6, 0, "O")
         product("m", 6, 1, "O")
         at_transpose(7)
-        early = (("L", 0, 0), ("L", 0, 1), ("L", 1, 0), ("T", 1, 1))
-        for tag, b, h in early:
-            product("x", b, h, tag, (0,))
-        at_copy(7, "S")
-        ch_copy("ac", attn_bf, 1, 0, "V")
-        residual("m", 6, 0)
+        early = ((0, 0), (0, 1), (1, 0), (1, 1))
+        for b, h in early:
+            product("x", b, h, "L", (0,))
+        ch_copy("ac", attn_bf, 1, 0, "V", 0, AC_SPLIT)
+        ch_copy("ac", attn_bf, 1, 0, "S", AC_SPLIT, HALF)
+        ch_copy("ac", attn_bf, 1, 1, "V", 0, AC_SPLIT)
+        ch_copy("ac", attn_bf, 1, 1, "S", AC_SPLIT, HALF)
         ch_quant("ac", DST["ac"], 1, 0)
-        ch_copy("ac", attn_bf, 1, 1, AC11)
+        residual("m", 6, 0)
         residual("m", 6, 1)
         store("m", 6)
+        at_copy(7, "S")
         at_quant(7)
-        for tag, b, h in early:
-            product("x", b, h, tag, (1,))
+        for b, h in early:
+            product("x", b, h, "L", (1,))
         product("m", 7, 0, "O")
         product("m", 7, 1, "O")
-        product("x", 2, 0, "T")
-        product("x", 2, 1, "O")
         order = [("x", 0), ("x", 1), ("m", 7)] + [("x", b) for b in range(2, 8)]
-        later_tags = (("L", "L"), ("L", "T"), ("O", "O"), ("T", "O"), ("L", "L"))
         for pos, (key, i) in enumerate(order):
             for h in range(2):
-                residual(key, i, h, "G" if (2 * pos + h) % 3 == GSEL and pos >= 1 else "V")
+                residual(key, i, h, "G" if (2 * pos + h) % 3 == GSEL and 1 <= pos <= 6 else "V")
                 if pos == len(order) - 1:
                     store(key, i, h * HALF, (h + 1) * HALF)
             if pos < len(order) - 1:
                 store(key, i)
             if pos == 0:
                 ch_quant("ac", DST["ac"], 1, 1)
-            if pos + 4 < len(order):
+            if pos + 3 < len(order):
                 for h in range(2):
-                    product("x", order[pos + 4][1], h, later_tags[pos][h])
+                    product("x", order[pos + 3][1], h, "L")

@@ -23,24 +23,14 @@ HALF = 512
 CH_BUFS = 5
 NORM = "G"
 GSEL = 2
-AC_SPLIT = 336
-V_HEAD = []
-HEAD_ENG = ("S", "V", "S", "V", "S", "V", "S", "V")
+AC_V = (160, 160, 160, 160)
+G_BANKS = (("x", 2, 1), ("x", 3, 1), ("m", 7, 1), ("x", 4, 1), ("x", 5, 1))
+SPLIT_STORES = (1, 9)
+CHUNKS = (("mc", 0, 0), ("mc", 0, 1), ("mc", 1, 0), ("mc", 1, 1), ("xc", 0, 0), ("xc", 0, 1), ("xc", 1, 0), ("xc", 1, 1), ("ac", 0, 0), ("ac", 0, 1))
+HEAD_ENG = ("S", "V", "S", "V", "S", "S", "S", "S")
+HEAD_V = {3: [("c", "mc", 0, 0, 0, 256)], 5: [("c", "mc", 0, 0, 256, 512)], 8: [("c", "mc", 0, 1, 0, 256)], 9: [("c", "mc", 0, 1, 256, 512)], 10: [("q", "mc", 0, 0)]}
 XT_AT = {0: [4, 5], 1: [6, 7]}
-V_FIRST = {0: [("xq", "", 2, 0)], 1: [("xq", "", 3, 0)], 2: [("xq", "", 4, 0)], 3: [("xq", "", 5, 0)], 4: [("xq", "", 6, 0)], 5: [("xq", "", 7, 0)]}
-V_EXTRA = {
-    0: [("c", "mc", 0, 1), ("c", "mc", 1, 0), ("q", "mc", 0, 1)],
-    1: [("q", "mc", 0, 0), ("c", "mc", 1, 1), ("q", "mc", 1, 0), ("q", "mc", 1, 1)],
-    2: [("c", "xc", 1, 1)],
-    3: [("q", "xc", 0, 0), ("q", "xc", 1, 1)],
-    4: [("c", "ac", 0, 0)],
-    5: [("q", "xc", 0, 1), ("q", "ac", 0, 0)],
-    6: [("c", "ac", 0, 1)],
-    7: [("q", "ac", 0, 1), ("q", "xc", 1, 0)],
-}
-S_EXTRA = {0: [("c0", "mc", 0, 0), ("c1", "mc", 0, 0), ("xc", "", 4, 0), ("xc", "", 5, 0)], 1: [("xc", "", 6, 0), ("xc", "", 7, 0), ("c0", "xc", 0, 0)],
-           2: [("c1", "xc", 0, 0)], 3: [("c0", "xc", 0, 1)], 4: [("c1", "xc", 0, 1)],
-           5: [("c0", "xc", 1, 0)], 6: [("c1", "xc", 1, 0)]}
+V_COLS = (512, 512, 160, 160, 160, 160, 160, 160)
 
 
 def tile_crossxmfusion_pa_kernel(tc, feature_x, feature_m, out_0, out_1):
@@ -161,8 +151,8 @@ def tile_crossxmfusion_pa_kernel(tc, feature_x, feature_m, out_0, out_1):
             copy_on(engine, st[key, g, half][:, lo:hi, :].rearrange("p (c i) j -> p c j i", i=4),
                     src[g][:, :, half * HALF + lo : half * HALF + hi].rearrange("p j (c i) -> p c j i", i=4))
 
-        def ch_quant(key, pair, g, half):
-            quantise(pair[0], pair[1], g * 1024 + half * HALF, st[key, g, half][:].rearrange("p c j -> p (c j)"))
+        def ch_quant(key, pair, g, half, lo=0, hi=HALF):
+            quantise(pair[0], pair[1], g * 1024 + half * HALF + lo, st[key, g, half][:, lo:hi, :].rearrange("p c j -> p (c j)"))
 
         attn_bf = [keep.tile([P, 4, C], BF16, name="attn_bf%d" % g, align_bytes=64) for g in range(2)]
 
@@ -255,19 +245,27 @@ def tile_crossxmfusion_pa_kernel(tc, feature_x, feature_m, out_0, out_1):
         DST = {"mc": (mc_codes, mc_scales), "xc": (xc_codes, xc_scales), "ac": (ac_codes, ac_scales)}
 
         def extras(items, engine):
-            for kind, key, g, half in items:
+            for item in items:
+                kind = item[0]
                 if kind == "c":
-                    ch_copy(key, SRC[key], g, half, engine)
-                elif kind == "c0":
-                    ch_copy(key, SRC[key], g, half, engine, 0, 256)
-                elif kind == "c1":
-                    ch_copy(key, SRC[key], g, half, engine, 256, 512)
+                    ch_copy(item[1], SRC[item[1]], item[2], item[3], engine, item[4], item[5])
                 elif kind == "q":
-                    ch_quant(key, DST[key], g, half)
+                    ch_quant(item[1], DST[item[1]], item[2], item[3])
                 elif kind == "xc":
-                    xt_copy(g, engine)
+                    xt_copy(item[1], engine)
                 else:
-                    xt_quant(g)
+                    xt_quant(item[1])
+
+        def chunk_copy(n, v_cols):
+            key, g, half = CHUNKS[n]
+            if v_cols > 0:
+                ch_copy(key, SRC[key], g, half, "V", 0, v_cols)
+            if v_cols < HALF:
+                ch_copy(key, SRC[key], g, half, "S", v_cols, HALF)
+
+        def chunk_quant(n):
+            key, g, half = CHUNKS[n]
+            ch_quant(key, DST[key], g, half)
 
         for i in range(8):
             mt_transpose(i, "T")
@@ -275,33 +273,37 @@ def tile_crossxmfusion_pa_kernel(tc, feature_x, feature_m, out_0, out_1):
             if i % 2 == 1:
                 mt_quant(i // 4, 0, (i % 4) // 2)
                 mt_quant(i // 4, 1, (i % 4) // 2)
+            extras(HEAD_V.get(i, []), "V")
         for i in range(4):
             xt_transpose(i, "T")
             xt_copy(i, "S")
             if i < 2:
                 xt_quant(i)
+            extras(HEAD_V.get(8 + i, []), "V")
         logits(0)
         logits(1)
-        extras(V_HEAD, "V")
         row_max(0)
         exps(0)
 
-        for k in range(0, 8):
+        for k in range(0, 7):
             if 0 <= k - 1:
                 at_transpose(k - 1)
             for i in XT_AT.get(k, []):
                 xt_transpose(i, "T")
             if 0 <= k - 2:
                 at_quant(k - 2)
+            chunk_quant(k + 1)
+            if 0 <= k - 2:
                 product("m", k - 2, 0, "O")
                 product("m", k - 2, 1, "O")
-            extras(V_FIRST.get(k, []), "V")
             if k + 2 < 8:
+                xt_quant(k + 2)
                 logits(k + 2)
             if 0 <= k - 1:
                 at_copy(k - 1, "S")
-            extras(V_EXTRA.get(k, []), "V")
-            extras(S_EXTRA.get(k, []), "S")
+            chunk_copy(k + 2, V_COLS[k])
+            for i in XT_AT.get(k, []):
+                xt_copy(i, "S")
             row_recip(k)
             normalise(k, NORM)
             if k + 1 < 8:
@@ -312,37 +314,74 @@ def tile_crossxmfusion_pa_kernel(tc, feature_x, feature_m, out_0, out_1):
                 residual("m", k - 2, 1)
                 store("m", k - 2)
 
-        at_quant(6)
-        product("m", 6, 0, "O")
-        product("m", 6, 1, "O")
-        at_transpose(7)
-        early = ((0, 0), (0, 1), (1, 0), (1, 1))
-        for b, h in early:
-            product("x", b, h, "L", (0,))
-        ch_copy("ac", attn_bf, 1, 0, "V", 0, AC_SPLIT)
-        ch_copy("ac", attn_bf, 1, 0, "S", AC_SPLIT, HALF)
-        ch_copy("ac", attn_bf, 1, 1, "V", 0, AC_SPLIT)
-        ch_copy("ac", attn_bf, 1, 1, "S", AC_SPLIT, HALF)
-        ch_quant("ac", DST["ac"], 1, 0)
-        residual("m", 6, 0)
-        residual("m", 6, 1)
-        store("m", 6)
-        at_copy(7, "S")
-        at_quant(7)
-        for b, h in early:
-            product("x", b, h, "L", (1,))
-        product("m", 7, 0, "O")
-        product("m", 7, 1, "O")
-        order = [("x", 0), ("x", 1), ("m", 7)] + [("x", b) for b in range(2, 8)]
-        for pos, (key, i) in enumerate(order):
+        def ac_copy(sub):
+            half, lo = sub // 2, 256 * (sub % 2)
+            v_cols = AC_V[sub]
+            if v_cols > 0:
+                ch_copy("ac", attn_bf, 1, half, "V", lo, lo + v_cols)
+            ch_copy("ac", attn_bf, 1, half, "S", lo + v_cols, lo + 256)
+
+        def ac_quant(sub):
+            half, lo = sub // 2, 256 * (sub % 2)
+            ch_quant("ac", DST["ac"], 1, half, lo, lo + 256)
+
+        def finish(key, i, split=False):
             for h in range(2):
-                residual(key, i, h, "G" if (2 * pos + h) % 3 == GSEL and 1 <= pos <= 6 else "V")
-                if pos == len(order) - 1:
+                residual(key, i, h, "G" if (key, i, h) in G_BANKS else "V")
+                if split:
                     store(key, i, h * HALF, (h + 1) * HALF)
-            if pos < len(order) - 1:
+            if not split:
                 store(key, i)
-            if pos == 0:
-                ch_quant("ac", DST["ac"], 1, 1)
-            if pos + 3 < len(order):
-                for h in range(2):
-                    product("x", order[pos + 3][1], h, "L")
+
+        def both(key, i, passes=(0, 1)):
+            product(key, i, 0, "L", passes)
+            product(key, i, 1, "L", passes)
+
+        at_transpose(6)
+        at_quant(5)
+        chunk_quant(8)
+        both("m", 5)
+        both("x", 0, (0,))
+        both("x", 1, (0,))
+        at_copy(6, "S")
+        row_recip(7)
+        normalise(7, "V")
+        at_transpose(7)
+        ac_copy(0)
+        ac_copy(1)
+        ac_quant(0)
+        residual("m", 5, 0)
+        ac_quant(1)
+        residual("m", 5, 1)
+        store("m", 5)
+        both("x", 0, (1,))
+        both("x", 1, (1,))
+        at_quant(6)
+        both("m", 6)
+        at_copy(7, "S")
+        chunk_copy(9, V_COLS[7])
+        product("x", 2, 0, "L")
+        ac_copy(2)
+        finish("x", 0, True)
+        product("x", 2, 1, "L")
+        product("x", 3, 0, "L")
+        ac_copy(3)
+        chunk_quant(9)
+        finish("x", 1)
+        product("x", 3, 1, "L")
+        at_quant(7)
+        both("m", 7)
+        ac_quant(2)
+        finish("m", 6)
+        both("x", 4)
+        ac_quant(3)
+        finish("x", 2)
+        both("x", 5)
+        finish("x", 3)
+        both("x", 6)
+        finish("m", 7)
+        both("x", 7)
+        finish("x", 4)
+        finish("x", 5)
+        finish("x", 6)
+        finish("x", 7, True)

@@ -23,12 +23,15 @@ HALF = 512
 CH_BUFS = 5
 NORM = "G"
 GSEL = 2
-AC_V = (160, 160, 160, 160)
+AC_V = (256, 128, 64, 64)
 G_BANKS = (("x", 2, 1), ("x", 3, 1), ("m", 7, 1), ("x", 4, 1), ("x", 5, 1))
 SPLIT_STORES = (1, 9)
 CHUNKS = (("mc", 0, 0), ("mc", 0, 1), ("mc", 1, 0), ("mc", 1, 1), ("xc", 0, 0), ("xc", 0, 1), ("xc", 1, 0), ("xc", 1, 1), ("ac", 0, 0), ("ac", 0, 1))
 HEAD_ENG = ("S", "V", "S", "V", "S", "S", "S", "S")
-HEAD_V = {3: [("c", "mc", 0, 0, 0, 256)], 5: [("c", "mc", 0, 0, 256, 512)], 8: [("c", "mc", 0, 1, 0, 256)], 9: [("c", "mc", 0, 1, 256, 512)], 10: [("q", "mc", 0, 0)]}
+HEAD_V = {3: [("c", "mc", 0, 0, 0, 256)], 5: [("c", "mc", 0, 0, 256, 512)], 8: [("c", "mc", 0, 1, 0, 256)], 10: [("q", "mc", 0, 0)]}
+HEAD_S = [("c", "mc", 0, 1, 256, 512)]
+G_COLS = 0
+SHIFT_AFTER = 1
 XT_AT = {0: [4, 5], 1: [6, 7]}
 V_COLS = (512, 512, 160, 160, 160, 160, 160, 160)
 
@@ -103,7 +106,9 @@ def tile_crossxmfusion_pa_kernel(tc, feature_x, feature_m, out_0, out_1):
             )
 
         def copy_on(engine, out, in_):
-            if engine == "S":
+            if engine == "G":
+                nc.gpsimd.tensor_scalar(out=out, in0=in_, scalar1=1.0, scalar2=0.0, op0=ALU.mult, op1=ALU.add)
+            elif engine == "S":
                 nc.scalar.copy(out=out, in_=in_)
             else:
                 nc.vector.tensor_copy(out=out, in_=in_)
@@ -146,7 +151,7 @@ def tile_crossxmfusion_pa_kernel(tc, feature_x, feature_m, out_0, out_1):
                      st["mtg", g][:, s * 2048 + pair * 1024 : s * 2048 + (pair + 1) * 1024])
 
         def ch_copy(key, src, g, half, engine, lo=0, hi=HALF):
-            if lo == 0:
+            if (key, g, half) not in st:
                 st[key, g, half] = stage.tile([P, HALF, 4], BF16, name="ch_g", bufs=CH_BUFS, align_bytes=64)
             copy_on(engine, st[key, g, half][:, lo:hi, :].rearrange("p (c i) j -> p c j i", i=4),
                     src[g][:, :, half * HALF + lo : half * HALF + hi].rearrange("p j (c i) -> p c j i", i=4))
@@ -167,6 +172,10 @@ def tile_crossxmfusion_pa_kernel(tc, feature_x, feature_m, out_0, out_1):
             mx2 = small.tile([P, 2], F32, name="mx2")
             for h in range(2):
                 nc.vector.tensor_reduce(out=mx2[:, h : h + 1], in_=st["lg", i][h][:], axis=AX.X, op=ALU.max)
+            st["mx2", i] = mx2
+
+        def row_shift(i):
+            mx2 = st["mx2", i]
             nb = small.tile([P, 1], F32, name="nb")
             nc.vector.tensor_scalar(out=nb[:], in0=mx2[:, 0:1], scalar1=mx2[:, 1:2], scalar2=-1.0 / T,
                                     op0=ALU.max, op1=ALU.mult)
@@ -258,10 +267,15 @@ def tile_crossxmfusion_pa_kernel(tc, feature_x, feature_m, out_0, out_1):
 
         def chunk_copy(n, v_cols):
             key, g, half = CHUNKS[n]
+            hi = HALF - (G_COLS if n >= 4 else 0)
             if v_cols > 0:
                 ch_copy(key, SRC[key], g, half, "V", 0, v_cols)
-            if v_cols < HALF:
-                ch_copy(key, SRC[key], g, half, "S", v_cols, HALF)
+            if v_cols < hi:
+                ch_copy(key, SRC[key], g, half, "S", v_cols, hi)
+
+        def chunk_copy_g(n):
+            key, g, half = CHUNKS[n]
+            ch_copy(key, SRC[key], g, half, "G", HALF - G_COLS, HALF)
 
         def chunk_quant(n):
             key, g, half = CHUNKS[n]
@@ -280,9 +294,11 @@ def tile_crossxmfusion_pa_kernel(tc, feature_x, feature_m, out_0, out_1):
             if i < 2:
                 xt_quant(i)
             extras(HEAD_V.get(8 + i, []), "V")
+        extras(HEAD_S, "S")
         logits(0)
         logits(1)
         row_max(0)
+        row_shift(0)
         exps(0)
 
         for k in range(0, 7):
@@ -306,12 +322,22 @@ def tile_crossxmfusion_pa_kernel(tc, feature_x, feature_m, out_0, out_1):
                 xt_copy(i, "S")
             row_recip(k)
             normalise(k, NORM)
+            if 4 <= k + 3 < 10 and G_COLS > 0:
+                chunk_copy_g(k + 3)
             if k + 1 < 8:
                 row_max(k + 1)
-                exps(k + 1)
-            if 0 <= k - 2:
+            if 0 <= k - 2 and SHIFT_AFTER >= 1:
                 residual("m", k - 2, 0)
+            if 0 <= k - 2 and SHIFT_AFTER >= 2:
                 residual("m", k - 2, 1)
+            if k + 1 < 8:
+                row_shift(k + 1)
+                exps(k + 1)
+            if 0 <= k - 2 and SHIFT_AFTER < 1:
+                residual("m", k - 2, 0)
+            if 0 <= k - 2 and SHIFT_AFTER < 2:
+                residual("m", k - 2, 1)
+            if 0 <= k - 2:
                 store("m", k - 2)
 
         def ac_copy(sub):
@@ -319,7 +345,8 @@ def tile_crossxmfusion_pa_kernel(tc, feature_x, feature_m, out_0, out_1):
             v_cols = AC_V[sub]
             if v_cols > 0:
                 ch_copy("ac", attn_bf, 1, half, "V", lo, lo + v_cols)
-            ch_copy("ac", attn_bf, 1, half, "S", lo + v_cols, lo + 256)
+            if v_cols < 256:
+                ch_copy("ac", attn_bf, 1, half, "S", lo + v_cols, lo + 256)
 
         def ac_quant(sub):
             half, lo = sub // 2, 256 * (sub % 2)

@@ -31,7 +31,9 @@ HEAD_ENG = ("S", "V", "S", "V", "S", "S", "S", "S")
 HEAD_V = {3: [("c", "mc", 0, 0, 0, 256)], 5: [("c", "mc", 0, 0, 256, 512)], 8: [("c", "mc", 0, 1, 0, 256)], 10: [("q", "mc", 0, 0)]}
 HEAD_S = [("c", "mc", 0, 1, 256, 512)]
 G_COLS = 0
-SHIFT_AFTER = 1
+SHIFT_AFTER = 0
+NB_ON_G = 0
+NORM_AT = {}
 XT_AT = {0: [4, 5], 1: [6, 7]}
 V_COLS = (512, 512, 160, 160, 160, 160, 160, 160)
 
@@ -176,9 +178,10 @@ def tile_crossxmfusion_pa_kernel(tc, feature_x, feature_m, out_0, out_1):
 
         def row_shift(i):
             mx2 = st["mx2", i]
+            mx1 = small.tile([P, 1], F32, name="mx1")
+            nc.vector.tensor_reduce(out=mx1[:], in_=mx2[:], axis=AX.X, op=ALU.max)
             nb = small.tile([P, 1], F32, name="nb")
-            nc.vector.tensor_scalar(out=nb[:], in0=mx2[:, 0:1], scalar1=mx2[:, 1:2], scalar2=-1.0 / T,
-                                    op0=ALU.max, op1=ALU.mult)
+            nc.scalar.mul(out=nb[:], in_=mx1[:], mul=-1.0 / T)
             st["nb", i] = nb
 
         def exps(i):
@@ -315,15 +318,13 @@ def tile_crossxmfusion_pa_kernel(tc, feature_x, feature_m, out_0, out_1):
             if k + 2 < 8:
                 xt_quant(k + 2)
                 logits(k + 2)
+            chunk_copy(k + 2, V_COLS[k])
             if 0 <= k - 1:
                 at_copy(k - 1, "S")
-            chunk_copy(k + 2, V_COLS[k])
             for i in XT_AT.get(k, []):
                 xt_copy(i, "S")
             row_recip(k)
-            normalise(k, NORM)
-            if 4 <= k + 3 < 10 and G_COLS > 0:
-                chunk_copy_g(k + 3)
+            normalise(k, NORM_AT.get(k, NORM))
             if k + 1 < 8:
                 row_max(k + 1)
             if 0 <= k - 2 and SHIFT_AFTER >= 1:
@@ -333,6 +334,8 @@ def tile_crossxmfusion_pa_kernel(tc, feature_x, feature_m, out_0, out_1):
             if k + 1 < 8:
                 row_shift(k + 1)
                 exps(k + 1)
+            if 4 <= k + 3 < 10 and G_COLS > 0:
+                chunk_copy_g(k + 3)
             if 0 <= k - 2 and SHIFT_AFTER < 1:
                 residual("m", k - 2, 0)
             if 0 <= k - 2 and SHIFT_AFTER < 2:

@@ -15,403 +15,324 @@ ACT = mybir.ActivationFunctionType
 AX = mybir.AxisListType
 
 P = 128
-C = 1024
-T = 1024
+N = 1024
 HALF = 512
-
-
-CH_BUFS = 5
-NORM = "G"
-GSEL = 2
-AC_V = (256, 128, 64, 64)
-G_BANKS = (("x", 2, 1), ("x", 3, 1), ("m", 7, 1), ("x", 4, 1), ("x", 5, 1))
-SPLIT_STORES = (1, 9)
-CHUNKS = (("mc", 0, 0), ("mc", 0, 1), ("mc", 1, 0), ("mc", 1, 1), ("xc", 0, 0), ("xc", 0, 1), ("xc", 1, 0), ("xc", 1, 1), ("ac", 0, 0), ("ac", 0, 1))
-HEAD_ENG = ("S", "V", "S", "V", "S", "S", "S", "S")
-HEAD_V = {3: [("c", "mc", 0, 0, 0, 256)], 5: [("c", "mc", 0, 0, 256, 512)], 8: [("c", "mc", 0, 1, 0, 256)], 10: [("q", "mc", 0, 0)]}
-HEAD_S = [("c", "mc", 0, 1, 256, 512)]
-G_COLS = 0
-SHIFT_AFTER = 0
-NB_ON_G = 0
-NORM_AT = {}
-XT_AT = {0: [4, 5], 1: [6, 7]}
-V_COLS = (512, 512, 160, 160, 160, 160, 160, 160)
+TILES = 8
+PIECE = 256
+VECTOR_SHARE = 160
 
 
 def tile_crossxmfusion_pa_kernel(tc, feature_x, feature_m, out_0, out_1):
     nc = tc.nc
-    xv = feature_x.flatten_outer_dims().rearrange("(g p j) t -> p g j t", g=2, j=4)
-    mv = feature_m.flatten_outer_dims().rearrange("(g p j) t -> p g j t", g=2, j=4)
-    o0v = out_0.flatten_outer_dims().rearrange("(g p j) t -> p g j t", g=2, j=4)
-    o1v = out_1.flatten_outer_dims().rearrange("(g p j) t -> p g j t", g=2, j=4)
+    by_tile = "(g p j) t -> p g j t"
+    x_dram = feature_x.flatten_outer_dims().rearrange(by_tile, g=2, j=4)
+    m_dram = feature_m.flatten_outer_dims().rearrange(by_tile, g=2, j=4)
+    out_dram = {
+        "x": out_0.flatten_outer_dims().rearrange(by_tile, g=2, j=4),
+        "m": out_1.flatten_outer_dims().rearrange(by_tile, g=2, j=4),
+    }
 
     with ExitStack() as ctx:
         keep = ctx.enter_context(tc.tile_pool(name="keep", bufs=1))
         stage = ctx.enter_context(tc.tile_pool(name="stage", bufs=2))
         small = ctx.enter_context(tc.tile_pool(name="small", bufs=4))
-        psum = ctx.enter_context(tc.psum_pool(name="psum", bufs=2))
+        psum = ctx.enter_context(tc.psum_pool(name="psum", bufs=8))
         ctx.enter_context(tc.manual_schedule())
 
         warm = small.tile([P, 2], F32, name="warm")
         nc.vector.memset(warm[:, 0:1], 0.0)
         nc.scalar.activation(out=warm[:, 1:2], in_=warm[:, 0:1], func=ACT.Exp)
 
-        ident_f = keep.tile([P, P], F32, name="ident_f")
-        make_identity(nc, ident_f[:])
-        ident_b = keep.tile([P, P], BF16, name="ident_b")
-        make_identity(nc, ident_b[:])
+        ident_f32 = keep.tile([P, P], F32, name="ident_f32")
+        make_identity(nc, ident_f32[:])
+        ident_bf16 = keep.tile([P, P], BF16, name="ident_bf16")
+        make_identity(nc, ident_bf16[:])
 
-        x_sb = [keep.tile([P, 4, T], BF16, name="x_sb%d" % g, align_bytes=64) for g in range(2)]
-        m_sb = [keep.tile([P, 4, T], BF16, name="m_sb%d" % g, align_bytes=64) for g in range(2)]
+        x_sb = [keep.tile([P, 4, N], BF16, name="x_sb%d" % g, align_bytes=64) for g in range(2)]
+        m_sb = [keep.tile([P, 4, N], BF16, name="m_sb%d" % g, align_bytes=64) for g in range(2)]
+        attn_sb = [keep.tile([P, 4, N], BF16, name="attn_sb%d" % g, align_bytes=64) for g in range(2)]
 
-        def load(dst, src, g, h):
-            nc.sync.dma_start(out=dst[g][:, 2 * h : 2 * h + 2, :], in_=src[:, g, 2 * h : 2 * h + 2, :])
+        def load(sb, dram, g, j0, j1):
+            nc.sync.dma_start(out=sb[g][:, j0:j1, :], in_=dram[:, g, j0:j1, :])
 
         for g in range(2):
-            for h in range(2):
-                load(m_sb, mv, g, h)
-        nc.sync.dma_start(out=x_sb[0][:, 0:1, :], in_=xv[:, 0, 0:1, :])
-        nc.sync.dma_start(out=x_sb[0][:, 1:4, :], in_=xv[:, 0, 1:4, :])
-        load(x_sb, xv, 1, 0)
-        load(x_sb, xv, 1, 1)
+            load(m_sb, m_dram, g, 0, 2)
+            load(m_sb, m_dram, g, 2, 4)
+        load(x_sb, x_dram, 0, 0, 1)
+        load(x_sb, x_dram, 0, 1, 4)
+        load(x_sb, x_dram, 1, 0, 2)
+        load(x_sb, x_dram, 1, 2, 4)
 
-        def codes_and_scales(name):
+        def operand(name):
             return (
-                keep.tile([P, 2048], U32, name=name + "_codes", align_bytes=64),
-                keep.tile([P, 2048], U8, name=name + "_scales", align_bytes=64),
+                keep.tile([P, 2 * N], U32, name=name + "_codes", align_bytes=64),
+                keep.tile([P, 2 * N], U8, name=name + "_scales", align_bytes=64),
             )
 
-        xt_codes, xt_scales = codes_and_scales("xt")
-        mt_codes, mt_scales = codes_and_scales("mt")
-        xc_codes, xc_scales = codes_and_scales("xc")
-        mc_codes, mc_scales = codes_and_scales("mc")
-        ac_codes, ac_scales = codes_and_scales("ac")
-        at_codes, at_scales = codes_and_scales("at")
+        x_t = operand("x_t")
+        m_t = operand("m_t")
+        attn_d = operand("attn_d")
+        by_channel = {"m": operand("m_c"), "x": operand("x_c"), "attn": operand("attn_c")}
+        plain = {"m": m_sb, "x": x_sb, "attn": attn_sb}
 
-        def quantise(codes, scales, start, grouped):
-            words = grouped.shape[1] // 4
-            nc.vector.quantize_mx(
-                out=codes[:, start : start + words].bitcast(FP8X4),
-                scales=scales[:, start : start + words],
-                in_=grouped,
-            )
+        def quantise(dst, start, grouped):
+            words = slice(start, start + grouped.shape[1] // 4)
+            nc.vector.quantize_mx(out=dst[0][:, words].bitcast(FP8X4), scales=dst[1][:, words], in_=grouped)
 
-        def mx(out, a, a_start, b, b_start, start, stop):
+        def mx_pass(acc, a, a_start, b, b_start, s):
+            a_cols = slice(a_start, a_start + P)
+            b_cols = slice(b_start, b_start + HALF)
             nc.tensor.matmul_mx(
-                out=out,
-                lhsT=a[0][:, a_start : a_start + P].bitcast(FP8X4),
-                lhsT_scale=a[1][:, a_start : a_start + P],
-                rhs=b[0][:, b_start : b_start + HALF].bitcast(FP8X4),
-                rhs_scale=b[1][:, b_start : b_start + HALF],
-                start=start,
-                stop=stop,
+                out=acc,
+                lhsT=a[0][:, a_cols].bitcast(FP8X4),
+                lhsT_scale=a[1][:, a_cols],
+                rhs=b[0][:, b_cols].bitcast(FP8X4),
+                rhs_scale=b[1][:, b_cols],
+                start=(s == 0),
+                stop=(s == 1),
             )
 
-        def copy_on(engine, out, in_):
-            if engine == "G":
-                nc.gpsimd.tensor_scalar(out=out, in0=in_, scalar1=1.0, scalar2=0.0, op0=ALU.mult, op1=ALU.add)
-            elif engine == "S":
-                nc.scalar.copy(out=out, in_=in_)
-            else:
-                nc.vector.tensor_copy(out=out, in_=in_)
+        def bank(shape, dtype):
+            return psum.tile(shape, dtype, name="bank")
 
-        def bank(tag, shape, dtype):
-            return psum.tile(shape, dtype, name="ps" + tag, tag="bank", bufs=8)
+        words_ps = {}
+        x_t_grouped = {}
+        m_t_grouped = {}
 
-        def transpose_words(row, tag):
-            words = row.bitcast(F32)
-            tw = bank(tag, [P, 4, P], F32)
+        def transpose_words(key, sb, i):
+            words = sb[i // 4][:, i % 4, :].bitcast(F32)
+            ps = bank([P, 4, P], F32)
             for b in range(4):
-                nc.tensor.transpose(tw[:, b, :], words[:, P * b : P * (b + 1)], ident_f[:])
-            return tw[:].rearrange("p (s u) c -> p s c u", s=2, u=2)
+                nc.tensor.transpose(ps[:, b, :], words[:, P * b : P * (b + 1)], ident_f32[:])
+            words_ps[key, i] = ps[:].rearrange("p (s u) c -> p s c u", s=2, u=2)
 
-        st = {}
+        def copy_x_t(i):
+            x_t_grouped[i] = stage.tile([P, N], BF16, name="x_t_grouped", bufs=6, align_bytes=64)
+            nc.scalar.copy(out=x_t_grouped[i][:].bitcast(F32).rearrange("p (s c u) -> p s c u", s=2, u=2),
+                           in_=words_ps["x", i])
 
-        def xt_transpose(i, tag):
-            st["xtp", i] = transpose_words(x_sb[i // 4][:, i % 4, :], tag)
+        def quantise_x_t(i):
+            quantise(x_t, 2 * P * i, x_t_grouped[i][:])
 
-        def xt_copy(i, engine):
-            xt_g = stage.tile([P, 1024], BF16, name="xt_g", bufs=6, align_bytes=64)
-            copy_on(engine, xt_g[:].bitcast(F32).rearrange("p (s c u) -> p s c u", s=2, u=2), st["xtp", i])
-            st["xtg", i] = xt_g
-
-        def xt_quant(i):
-            quantise(xt_codes, xt_scales, i * 256, st["xtg", i][:])
-
-        def mt_transpose(i, tag):
-            st["mtp", i] = transpose_words(m_sb[i // 4][:, i % 4, :], tag)
-
-        def mt_copy(i, engine):
+        def copy_m_t(copy, i):
             g, j = divmod(i, 4)
             if j == 0:
-                st["mtg", g] = stage.tile([P, 4096], BF16, name="mt_g", bufs=2, align_bytes=64)
-            view = st["mtg", g][:].bitcast(F32).rearrange("p (s n u) -> p s n u", s=2, u=2)
-            copy_on(engine, view[:, :, P * j : P * (j + 1), :], st["mtp", i])
+                m_t_grouped[g] = stage.tile([P, 4 * N], BF16, name="m_t_grouped", bufs=2, align_bytes=64)
+            view = m_t_grouped[g][:].bitcast(F32).rearrange("p (s n u) -> p s n u", s=2, u=2)
+            copy(out=view[:, :, P * j : P * (j + 1), :], in_=words_ps["m", i])
 
-        def mt_quant(g, s, pair):
-            quantise(mt_codes, mt_scales, s * 1024 + g * HALF + pair * 256,
-                     st["mtg", g][:, s * 2048 + pair * 1024 : s * 2048 + (pair + 1) * 1024])
+        def quantise_m_t(g, pair):
+            for s in range(2):
+                quantise(m_t, s * N + g * HALF + pair * PIECE,
+                         m_t_grouped[g][:, s * 2 * N + pair * N : s * 2 * N + (pair + 1) * N])
 
-        def ch_copy(key, src, g, half, engine, lo=0, hi=HALF):
-            if (key, g, half) not in st:
-                st[key, g, half] = stage.tile([P, HALF, 4], BF16, name="ch_g", bufs=CH_BUFS, align_bytes=64)
-            copy_on(engine, st[key, g, half][:, lo:hi, :].rearrange("p (c i) j -> p c j i", i=4),
-                    src[g][:, :, half * HALF + lo : half * HALF + hi].rearrange("p j (c i) -> p c j i", i=4))
+        chunks = [("m", g, h) for g in range(2) for h in range(2)]
+        chunks += [("x", g, h) for g in range(2) for h in range(2)]
+        chunks += [("attn", g, h) for g in range(2) for h in range(2)]
+        chunk_grouped = {}
 
-        def ch_quant(key, pair, g, half, lo=0, hi=HALF):
-            quantise(pair[0], pair[1], g * 1024 + half * HALF + lo, st[key, g, half][:, lo:hi, :].rearrange("p c j -> p (c j)"))
+        def regroup(copy, n, lo, hi):
+            name, g, h = chunks[n]
+            if n not in chunk_grouped:
+                chunk_grouped[n] = stage.tile([P, HALF, 4], BF16, name="chunk_grouped", bufs=5, align_bytes=64)
+            copy(out=chunk_grouped[n][:, lo:hi, :].rearrange("p (c i) j -> p c j i", i=4),
+                 in_=plain[name][g][:, :, h * HALF + lo : h * HALF + hi].rearrange("p j (c i) -> p c j i", i=4))
 
-        attn_bf = [keep.tile([P, 4, C], BF16, name="attn_bf%d" % g, align_bytes=64) for g in range(2)]
+        def quantise_chunk(n, lo=0, hi=HALF):
+            name, g, h = chunks[n]
+            quantise(by_channel[name], g * N + h * HALF + lo,
+                     chunk_grouped[n][:, lo:hi, :].rearrange("p c j -> p (c j)"))
+
+        logits_ps = {}
+        half_max = {}
+        shift = {}
+        exp_sb = {}
+        half_sum = {}
+        inv_sum = {}
 
         def logits(i):
-            st["lg", i] = [bank("L", [P, HALF], F32) for h in range(2)]
+            logits_ps[i] = [bank([P, HALF], F32) for h in range(2)]
             for h in range(2):
                 for s in range(2):
-                    mx(st["lg", i][h][:], (xt_codes, xt_scales), i * 256 + s * P,
-                       (mt_codes, mt_scales), s * 1024 + h * HALF, s == 0, s == 1)
+                    mx_pass(logits_ps[i][h][:], x_t, 2 * P * i + s * P, m_t, s * N + h * HALF, s)
 
         def row_max(i):
-            mx2 = small.tile([P, 2], F32, name="mx2")
+            half_max[i] = small.tile([P, 2], F32, name="half_max")
             for h in range(2):
-                nc.vector.tensor_reduce(out=mx2[:, h : h + 1], in_=st["lg", i][h][:], axis=AX.X, op=ALU.max)
-            st["mx2", i] = mx2
+                nc.vector.tensor_reduce(out=half_max[i][:, h : h + 1], in_=logits_ps[i][h][:], axis=AX.X, op=ALU.max)
 
         def row_shift(i):
-            mx2 = st["mx2", i]
-            mx1 = small.tile([P, 1], F32, name="mx1")
-            nc.vector.tensor_reduce(out=mx1[:], in_=mx2[:], axis=AX.X, op=ALU.max)
-            nb = small.tile([P, 1], F32, name="nb")
-            nc.scalar.mul(out=nb[:], in_=mx1[:], mul=-1.0 / T)
-            st["nb", i] = nb
+            shift[i] = small.tile([P, 1], F32, name="shift")
+            nc.vector.tensor_scalar(out=shift[i][:], in0=half_max[i][:, 0:1], scalar1=half_max[i][:, 1:2],
+                                    scalar2=-1.0 / N, op0=ALU.max, op1=ALU.mult)
 
-        def exps(i):
-            e = stage.tile([P, C], F32, name="e", bufs=3)
-            s2 = small.tile([P, 2], F32, name="s2")
+        def exponentials(i):
+            exp_sb[i] = stage.tile([P, N], F32, name="exp_sb", bufs=3)
+            half_sum[i] = small.tile([P, 2], F32, name="half_sum")
             for h in range(2):
-                nc.scalar.activation(out=e[:, h * HALF : (h + 1) * HALF], in_=st["lg", i][h][:], func=ACT.Exp,
-                                     bias=st["nb", i][:], scale=1.0 / T, accum_out=s2[:, h : h + 1])
-            st["e", i] = e
-            st["s2", i] = s2
+                nc.scalar.activation(out=exp_sb[i][:, h * HALF : (h + 1) * HALF], in_=logits_ps[i][h][:], func=ACT.Exp,
+                                     bias=shift[i][:], scale=1.0 / N, accum_out=half_sum[i][:, h : h + 1])
 
-        def row_recip(i):
-            s2 = st["s2", i]
-            ssum = small.tile([P, 1], F32, name="ssum")
-            nc.vector.tensor_scalar(out=ssum[:], in0=s2[:, 0:1], scalar1=s2[:, 1:2], scalar2=None, op0=ALU.add)
-            r = small.tile([P, 1], F32, name="r")
-            nc.vector.reciprocal(out=r[:], in_=ssum[:])
-            st["r", i] = r
+        def reciprocal(i):
+            row_sum = small.tile([P, 1], F32, name="row_sum")
+            nc.vector.tensor_scalar(out=row_sum[:], in0=half_sum[i][:, 0:1], scalar1=half_sum[i][:, 1:2],
+                                    scalar2=None, op0=ALU.add)
+            inv_sum[i] = small.tile([P, 1], F32, name="inv_sum")
+            nc.vector.reciprocal(out=inv_sum[i][:], in_=row_sum[:])
 
-        def normalise(i, engine):
-            out = attn_bf[i // 4][:, i % 4, :]
-            if engine == "S":
-                nc.scalar.activation(out=out, in_=st["e", i][:], func=ACT.Copy, scale=st["r", i][:])
-            elif engine == "V":
-                nc.vector.tensor_scalar(out=out, in0=st["e", i][:], scalar1=st["r", i][:], scalar2=None, op0=ALU.mult)
-            else:
-                nc.gpsimd.tensor_scalar(out=out, in0=st["e", i][:], scalar1=st["r", i][:], scalar2=0.0,
-                                        op0=ALU.mult, op1=ALU.add)
+        attn_t_ps = {}
+        attn_d_grouped = {}
 
-        def at_transpose(i):
-            at_ps = bank("T", [P, 8, P], BF16)
+        def transpose_attn(i):
+            attn_t_ps[i] = bank([P, 8, P], BF16)
             for b in range(8):
-                nc.tensor.transpose(at_ps[:, b, :], attn_bf[i // 4][:, i % 4, P * b : P * (b + 1)], ident_b[:])
-            st["atp", i] = at_ps
+                nc.tensor.transpose(attn_t_ps[i][:, b, :], attn_sb[i // 4][:, i % 4, P * b : P * (b + 1)], ident_bf16[:])
 
-        def at_copy(i, engine):
-            at_g = stage.tile([P, 1024], BF16, name="at_g", bufs=3, align_bytes=64)
-            copy_on(engine, at_g[:].rearrange("p (s c k) -> p s c k", s=2, k=4),
-                    st["atp", i][:].rearrange("p (s k) c -> p s c k", s=2, k=4))
-            st["atg", i] = at_g
+        def copy_attn_d(i):
+            attn_d_grouped[i] = stage.tile([P, N], BF16, name="attn_d_grouped", bufs=3, align_bytes=64)
+            nc.scalar.copy(out=attn_d_grouped[i][:].rearrange("p (s c k) -> p s c k", s=2, k=4),
+                           in_=attn_t_ps[i][:].rearrange("p (s k) c -> p s c k", s=2, k=4))
 
-        def at_quant(i):
-            quantise(at_codes, at_scales, i * 256, st["atg", i][:])
+        def quantise_attn_d(i):
+            quantise(attn_d, 2 * P * i, attn_d_grouped[i][:])
 
-        def product(key, i, h, tag, passes=(0, 1)):
-            if passes[0] == 0:
-                st["acc", key, i, h] = bank(tag, [P, HALF], F32)
-            acc = st["acc", key, i, h]
-            for s in passes:
-                if key == "m":
-                    mx(acc[:], (at_codes, at_scales), i * 256 + s * P, (mc_codes, mc_scales), s * 1024 + h * HALF, s == 0, s == 1)
-                else:
-                    mx(acc[:], (ac_codes, ac_scales), s * 1024 + i * P, (xc_codes, xc_scales), s * 1024 + h * HALF, s == 0, s == 1)
+        acc_ps = {}
+        result = {}
 
-        def residual(key, i, h, engine="V"):
-            g, j = divmod(i, 4)
+        def product(name, i, passes=(0, 1)):
+            for h in range(2):
+                if passes[0] == 0:
+                    acc_ps[name, i, h] = bank([P, HALF], F32)
+                for s in passes:
+                    if name == "m":
+                        mx_pass(acc_ps[name, i, h][:], attn_d, 2 * P * i + s * P, by_channel["m"], s * N + h * HALF, s)
+                    else:
+                        mx_pass(acc_ps[name, i, h][:], by_channel["attn"], s * N + i * P, by_channel["x"], s * N + h * HALF, s)
+
+        def add_residual(name, i, h, by_gpsimd=False):
             if h == 0:
-                st["res", key, i] = stage.tile([P, T], F32, name="res", bufs=6)
-            res = st["res", key, i]
-            src = (m_sb if key == "m" else x_sb)[g]
+                result[name, i] = stage.tile([P, N], F32, name="result", bufs=6)
             cols = slice(h * HALF, (h + 1) * HALF)
-            if engine == "V":
-                nc.vector.tensor_tensor(out=res[:, cols], in0=st["acc", key, i, h][:], in1=src[:, j, cols], op=ALU.add)
+            out = result[name, i][:, cols]
+            residual = plain[name][i // 4][:, i % 4, cols]
+            if by_gpsimd:
+                nc.scalar.copy(out=out, in_=acc_ps[name, i, h][:])
+                nc.gpsimd.tensor_tensor(out=out, in0=out, in1=residual, op=ALU.add)
             else:
-                nc.scalar.copy(out=res[:, cols], in_=st["acc", key, i, h][:])
-                nc.gpsimd.tensor_tensor(out=res[:, cols], in0=res[:, cols], in1=src[:, j, cols], op=ALU.add)
+                nc.vector.tensor_tensor(out=out, in0=acc_ps[name, i, h][:], in1=residual, op=ALU.add)
 
-        def store(key, i, lo=0, hi=T):
-            g, j = divmod(i, 4)
-            nc.sync.dma_start(out=(o1v if key == "m" else o0v)[:, g, j, lo:hi], in_=st["res", key, i][:, lo:hi])
+        def store(name, i, lo=0, hi=N):
+            nc.sync.dma_start(out=out_dram[name][:, i // 4, i % 4, lo:hi], in_=result[name, i][:, lo:hi])
 
-        SRC = {"mc": m_sb, "xc": x_sb, "ac": attn_bf}
-        DST = {"mc": (mc_codes, mc_scales), "xc": (xc_codes, xc_scales), "ac": (ac_codes, ac_scales)}
-
-        def extras(items, engine):
-            for item in items:
-                kind = item[0]
-                if kind == "c":
-                    ch_copy(item[1], SRC[item[1]], item[2], item[3], engine, item[4], item[5])
-                elif kind == "q":
-                    ch_quant(item[1], DST[item[1]], item[2], item[3])
-                elif kind == "xc":
-                    xt_copy(item[1], engine)
-                else:
-                    xt_quant(item[1])
-
-        def chunk_copy(n, v_cols):
-            key, g, half = CHUNKS[n]
-            hi = HALF - (G_COLS if n >= 4 else 0)
-            if v_cols > 0:
-                ch_copy(key, SRC[key], g, half, "V", 0, v_cols)
-            if v_cols < hi:
-                ch_copy(key, SRC[key], g, half, "S", v_cols, hi)
-
-        def chunk_copy_g(n):
-            key, g, half = CHUNKS[n]
-            ch_copy(key, SRC[key], g, half, "G", HALF - G_COLS, HALF)
-
-        def chunk_quant(n):
-            key, g, half = CHUNKS[n]
-            ch_quant(key, DST[key], g, half)
-
-        for i in range(8):
-            mt_transpose(i, "T")
-            mt_copy(i, HEAD_ENG[i])
+        for i in range(TILES):
+            transpose_words("m", m_sb, i)
+            copy_m_t(nc.vector.tensor_copy if i in (1, 3) else nc.scalar.copy, i)
             if i % 2 == 1:
-                mt_quant(i // 4, 0, (i % 4) // 2)
-                mt_quant(i // 4, 1, (i % 4) // 2)
-            extras(HEAD_V.get(i, []), "V")
+                quantise_m_t(i // 4, (i % 4) // 2)
+            if i in (3, 5):
+                regroup(nc.vector.tensor_copy, 0, PIECE * (i // 5), PIECE * (i // 5 + 1))
         for i in range(4):
-            xt_transpose(i, "T")
-            xt_copy(i, "S")
+            transpose_words("x", x_sb, i)
+            copy_x_t(i)
             if i < 2:
-                xt_quant(i)
-            extras(HEAD_V.get(8 + i, []), "V")
-        extras(HEAD_S, "S")
+                quantise_x_t(i)
+            if i == 0:
+                regroup(nc.vector.tensor_copy, 1, 0, PIECE)
+        quantise_chunk(0)
+        regroup(nc.scalar.copy, 1, PIECE, HALF)
         logits(0)
         logits(1)
         row_max(0)
         row_shift(0)
-        exps(0)
+        exponentials(0)
 
-        for k in range(0, 7):
-            if 0 <= k - 1:
-                at_transpose(k - 1)
-            for i in XT_AT.get(k, []):
-                xt_transpose(i, "T")
-            if 0 <= k - 2:
-                at_quant(k - 2)
-            chunk_quant(k + 1)
-            if 0 <= k - 2:
-                product("m", k - 2, 0, "O")
-                product("m", k - 2, 1, "O")
-            if k + 2 < 8:
-                xt_quant(k + 2)
+        for k in range(TILES - 1):
+            late_x = (4 + 2 * k, 5 + 2 * k) if k < 2 else ()
+            if k >= 1:
+                transpose_attn(k - 1)
+            for i in late_x:
+                transpose_words("x", x_sb, i)
+            if k >= 2:
+                quantise_attn_d(k - 2)
+            quantise_chunk(k + 1)
+            if k >= 2:
+                product("m", k - 2)
+            if k + 2 < TILES:
+                quantise_x_t(k + 2)
                 logits(k + 2)
-            chunk_copy(k + 2, V_COLS[k])
-            if 0 <= k - 1:
-                at_copy(k - 1, "S")
-            for i in XT_AT.get(k, []):
-                xt_copy(i, "S")
-            row_recip(k)
-            normalise(k, NORM_AT.get(k, NORM))
-            if k + 1 < 8:
-                row_max(k + 1)
-            if 0 <= k - 2 and SHIFT_AFTER >= 1:
-                residual("m", k - 2, 0)
-            if 0 <= k - 2 and SHIFT_AFTER >= 2:
-                residual("m", k - 2, 1)
-            if k + 1 < 8:
-                row_shift(k + 1)
-                exps(k + 1)
-            if 4 <= k + 3 < 10 and G_COLS > 0:
-                chunk_copy_g(k + 3)
-            if 0 <= k - 2 and SHIFT_AFTER < 1:
-                residual("m", k - 2, 0)
-            if 0 <= k - 2 and SHIFT_AFTER < 2:
-                residual("m", k - 2, 1)
-            if 0 <= k - 2:
+            share = VECTOR_SHARE if k >= 2 else HALF
+            regroup(nc.vector.tensor_copy, k + 2, 0, share)
+            if share < HALF:
+                regroup(nc.scalar.copy, k + 2, share, HALF)
+            if k >= 1:
+                copy_attn_d(k - 1)
+            for i in late_x:
+                copy_x_t(i)
+            reciprocal(k)
+            nc.gpsimd.tensor_scalar(out=attn_sb[k // 4][:, k % 4, :], in0=exp_sb[k][:], scalar1=inv_sum[k][:],
+                                    scalar2=0.0, op0=ALU.mult, op1=ALU.add)
+            row_max(k + 1)
+            if k >= 2:
+                add_residual("m", k - 2, 0)
+            row_shift(k + 1)
+            exponentials(k + 1)
+            if k >= 2:
+                add_residual("m", k - 2, 1)
                 store("m", k - 2)
 
-        def ac_copy(sub):
-            half, lo = sub // 2, 256 * (sub % 2)
-            v_cols = AC_V[sub]
-            if v_cols > 0:
-                ch_copy("ac", attn_bf, 1, half, "V", lo, lo + v_cols)
-            if v_cols < 256:
-                ch_copy("ac", attn_bf, 1, half, "S", lo + v_cols, lo + 256)
+        last = TILES - 1
 
-        def ac_quant(sub):
-            half, lo = sub // 2, 256 * (sub % 2)
-            ch_quant("ac", DST["ac"], 1, half, lo, lo + 256)
+        def regroup_piece(copy, q, lo=0, hi=PIECE):
+            regroup(copy, 10 + q // 2, PIECE * (q % 2) + lo, PIECE * (q % 2) + hi)
 
-        def finish(key, i, split=False):
+        def quantise_piece(q):
+            quantise_chunk(10 + q // 2, PIECE * (q % 2), PIECE * (q % 2 + 1))
+
+        jobs = []
+        for n in range(3):
+            jobs += [("m", last - 2 + n), ("x", 2 * n), ("x", 2 * n + 1)]
+        jobs += [("x", 6), ("x", 7)]
+
+        transpose_attn(last - 1)
+        quantise_attn_d(last - 2)
+        quantise_chunk(8)
+        product("m", last - 2)
+        product("x", 0, (0,))
+        product("x", 1, (0,))
+        copy_attn_d(last - 1)
+        reciprocal(last)
+        nc.vector.tensor_scalar(out=attn_sb[last // 4][:, last % 4, :], in0=exp_sb[last][:], scalar1=inv_sum[last][:],
+                                scalar2=None, op0=ALU.mult)
+        transpose_attn(last)
+        regroup_piece(nc.vector.tensor_copy, 0)
+        regroup_piece(nc.vector.tensor_copy, 1)
+        regroup(nc.scalar.copy, 9, 0, HALF)
+        copy_attn_d(last)
+        regroup_piece(nc.scalar.copy, 2)
+        regroup_piece(nc.scalar.copy, 3)
+
+        def prepare(name, i):
+            if name == "m":
+                quantise_attn_d(i)
+            elif i % 2 == 0:
+                if i == 4:
+                    quantise_chunk(9)
+                quantise_piece(i // 2)
+
+        prepare("x", 0)
+        product("x", 0, (1,))
+        product("x", 1, (1,))
+        prepare("m", last - 1)
+        prepare("x", 2)
+        for n, (name, i) in enumerate(jobs):
+            halves = n == 1 or n == len(jobs) - 1
             for h in range(2):
-                residual(key, i, h, "G" if (key, i, h) in G_BANKS else "V")
-                if split:
-                    store(key, i, h * HALF, (h + 1) * HALF)
-            if not split:
-                store(key, i)
-
-        def both(key, i, passes=(0, 1)):
-            product(key, i, 0, "L", passes)
-            product(key, i, 1, "L", passes)
-
-        at_transpose(6)
-        at_quant(5)
-        chunk_quant(8)
-        both("m", 5)
-        both("x", 0, (0,))
-        both("x", 1, (0,))
-        at_copy(6, "S")
-        row_recip(7)
-        normalise(7, "V")
-        at_transpose(7)
-        ac_copy(0)
-        ac_copy(1)
-        ac_quant(0)
-        residual("m", 5, 0)
-        ac_quant(1)
-        residual("m", 5, 1)
-        store("m", 5)
-        both("x", 0, (1,))
-        both("x", 1, (1,))
-        at_quant(6)
-        both("m", 6)
-        at_copy(7, "S")
-        chunk_copy(9, V_COLS[7])
-        product("x", 2, 0, "L")
-        ac_copy(2)
-        finish("x", 0, True)
-        product("x", 2, 1, "L")
-        product("x", 3, 0, "L")
-        ac_copy(3)
-        chunk_quant(9)
-        finish("x", 1)
-        product("x", 3, 1, "L")
-        at_quant(7)
-        both("m", 7)
-        ac_quant(2)
-        finish("m", 6)
-        both("x", 4)
-        ac_quant(3)
-        finish("x", 2)
-        both("x", 5)
-        finish("x", 3)
-        both("x", 6)
-        finish("m", 7)
-        both("x", 7)
-        finish("x", 4)
-        finish("x", 5)
-        finish("x", 6)
-        finish("x", 7, True)
+                add_residual(name, i, h, by_gpsimd=(h == 1 and 4 <= n <= 8))
+                if halves:
+                    store(name, i, h * HALF, (h + 1) * HALF)
+            if not halves:
+                store(name, i)
+            if n + 5 < len(jobs):
+                prepare(jobs[n + 5][0], jobs[n + 5][1])
+            if n + 3 < len(jobs):
+                product(jobs[n + 3][0], jobs[n + 3][1])

@@ -19,7 +19,6 @@ N = 1024
 HALF = 512
 TILES = 8
 PIECE = 256
-VECTOR_SHARE = 160
 
 
 def tile_crossxmfusion_pa_kernel(tc, feature_x, feature_m, out_0, out_1):
@@ -45,8 +44,6 @@ def tile_crossxmfusion_pa_kernel(tc, feature_x, feature_m, out_0, out_1):
 
         ident_f32 = keep.tile([P, P], F32, name="ident_f32")
         make_identity(nc, ident_f32[:])
-        ident_bf16 = keep.tile([P, P], BF16, name="ident_bf16")
-        make_identity(nc, ident_bf16[:])
 
         x_sb = [keep.tile([P, 4, N], BF16, name="x_sb%d" % g, align_bytes=64) for g in range(2)]
         m_sb = [keep.tile([P, 4, N], BF16, name="m_sb%d" % g, align_bytes=64) for g in range(2)]
@@ -114,17 +111,22 @@ def tile_crossxmfusion_pa_kernel(tc, feature_x, feature_m, out_0, out_1):
         def quantise_x_t(i):
             quantise(x_t, 2 * P * i, x_t_grouped[i][:])
 
-        def copy_m_t(copy, i):
-            g, j = divmod(i, 4)
-            if j == 0:
-                m_t_grouped[g] = stage.tile([P, 4 * N], BF16, name="m_t_grouped", bufs=2, align_bytes=64)
-            view = m_t_grouped[g][:].bitcast(F32).rearrange("p (s n u) -> p s n u", s=2, u=2)
-            copy(out=view[:, :, P * j : P * (j + 1), :], in_=words_ps["m", i])
+        def transpose_m_words(g, u, s):
+            ps = bank([P, 2, 2, P], F32)
+            for e in range(2):
+                words = m_sb[g][:, 2 * u + e, :].bitcast(F32)
+                for v in range(2):
+                    b = 2 * s + v
+                    nc.tensor.transpose(ps[:, e, v, :], words[:, P * b : P * (b + 1)], ident_f32[:])
+            words_ps["m", g, u, s] = ps[:].rearrange("p e v c -> p c e v")
 
-        def quantise_m_t(g, pair):
-            for s in range(2):
-                quantise(m_t, s * N + g * HALF + pair * PIECE,
-                         m_t_grouped[g][:, s * 2 * N + pair * N : s * 2 * N + (pair + 1) * N])
+        def copy_m_t(copy, g, u, s):
+            m_t_grouped[g, u, s] = stage.tile([P, N], BF16, name="m_t_grouped", bufs=8, align_bytes=64)
+            copy(out=m_t_grouped[g, u, s][:].bitcast(F32).rearrange("p (c e v) -> p c e v", e=2, v=2),
+                 in_=words_ps["m", g, u, s])
+
+        def quantise_m_t(g, u, s):
+            quantise(m_t, s * N + g * HALF + u * PIECE, m_t_grouped[g, u, s][:])
 
         chunks = [("m", g, h) for g in range(2) for h in range(2)]
         chunks += [("x", g, h) for g in range(2) for h in range(2)]
@@ -135,6 +137,16 @@ def tile_crossxmfusion_pa_kernel(tc, feature_x, feature_m, out_0, out_1):
             name, g, h = chunks[n]
             if n not in chunk_grouped:
                 chunk_grouped[n] = stage.tile([P, HALF, 4], BF16, name="chunk_grouped", bufs=5, align_bytes=64)
+            if name == "attn":
+                for c0 in range(lo, hi, P):
+                    u, e = divmod(c0 // P, 2)
+                    start = h * HALF + u * PIECE
+                    pairs = attn_sb[g][:, :, start : start + PIECE].rearrange("p j (c e) -> p e c j", e=2)
+                    if e == 0 and hi - c0 >= PIECE:
+                        copy(out=chunk_grouped[n][:, c0 : c0 + PIECE, :].rearrange("p (e c) j -> p e c j", e=2), in_=pairs)
+                    elif e == 0 or c0 == lo:
+                        copy(out=chunk_grouped[n][:, c0 : c0 + P, :], in_=pairs[:, e, :, :])
+                return
             copy(out=chunk_grouped[n][:, lo:hi, :].rearrange("p (c i) j -> p c j i", i=4),
                  in_=plain[name][g][:, :, h * HALF + lo : h * HALF + hi].rearrange("p j (c i) -> p c j i", i=4))
 
@@ -184,14 +196,16 @@ def tile_crossxmfusion_pa_kernel(tc, feature_x, feature_m, out_0, out_1):
         attn_d_grouped = {}
 
         def transpose_attn(i):
-            attn_t_ps[i] = bank([P, 8, P], BF16)
-            for b in range(8):
-                nc.tensor.transpose(attn_t_ps[i][:, b, :], attn_sb[i // 4][:, i % 4, P * b : P * (b + 1)], ident_bf16[:])
+            words = attn_sb[i // 4][:, i % 4, :].bitcast(F32)
+            ps = bank([P, 4, P], F32)
+            for b in range(4):
+                nc.tensor.transpose(ps[:, b, :], words[:, P * b : P * (b + 1)], ident_f32[:])
+            attn_t_ps[i] = ps[:].rearrange("p (s u) c -> p s c u", s=2, u=2)
 
         def copy_attn_d(i):
             attn_d_grouped[i] = stage.tile([P, N], BF16, name="attn_d_grouped", bufs=3, align_bytes=64)
-            nc.scalar.copy(out=attn_d_grouped[i][:].rearrange("p (s c k) -> p s c k", s=2, k=4),
-                           in_=attn_t_ps[i][:].rearrange("p (s k) c -> p s c k", s=2, k=4))
+            nc.scalar.copy(out=attn_d_grouped[i][:].bitcast(F32).rearrange("p (s c u) -> p s c u", s=2, u=2),
+                           in_=attn_t_ps[i])
 
         def quantise_attn_d(i):
             quantise(attn_d, 2 * P * i, attn_d_grouped[i][:])
@@ -211,7 +225,7 @@ def tile_crossxmfusion_pa_kernel(tc, feature_x, feature_m, out_0, out_1):
 
         def add_residual(name, i, h, by_gpsimd=False):
             if h == 0:
-                result[name, i] = stage.tile([P, N], F32, name="result", bufs=6)
+                result[name, i] = stage.tile([P, N], F32, name="result", bufs=12)
             cols = slice(h * HALF, (h + 1) * HALF)
             out = result[name, i][:, cols]
             residual = plain[name][i // 4][:, i % 4, cols]
@@ -224,13 +238,23 @@ def tile_crossxmfusion_pa_kernel(tc, feature_x, feature_m, out_0, out_1):
         def store(name, i, lo=0, hi=N):
             nc.sync.dma_start(out=out_dram[name][:, i // 4, i % 4, lo:hi], in_=result[name, i][:, lo:hi])
 
-        for i in range(TILES):
-            transpose_words("m", m_sb, i)
-            copy_m_t(nc.vector.tensor_copy if i in (1, 3) else nc.scalar.copy, i)
-            if i % 2 == 1:
-                quantise_m_t(i // 4, (i % 4) // 2)
-            if i in (3, 5):
-                regroup(nc.vector.tensor_copy, 0, PIECE * (i // 5), PIECE * (i // 5 + 1))
+        V, S = nc.vector.tensor_copy, nc.scalar.copy
+
+        def normalise(k):
+            reciprocal(k)
+            nc.gpsimd.tensor_scalar(out=attn_sb[k // 4][:, k % 4, :], in0=exp_sb[k][:], scalar1=inv_sum[k][:],
+                                    scalar2=0.0, op0=ALU.mult, op1=ALU.add)
+
+        for q in range(4):
+            g, u = divmod(q, 2)
+            for s in range(2):
+                transpose_m_words(g, u, s)
+            for s in range(2):
+                copy_m_t(nc.vector.tensor_copy if s == 1 and q in (0, 3) else nc.scalar.copy, g, u, s)
+            for s in range(2):
+                quantise_m_t(g, u, s)
+            if q in (1, 2):
+                regroup(nc.vector.tensor_copy, 0, PIECE * (q // 2), PIECE * (q // 2 + 1))
         for i in range(4):
             transpose_words("x", x_sb, i)
             copy_x_t(i)
@@ -246,7 +270,7 @@ def tile_crossxmfusion_pa_kernel(tc, feature_x, feature_m, out_0, out_1):
         row_shift(0)
         exponentials(0)
 
-        for k in range(TILES - 1):
+        for k in range(TILES - 2):
             late_x = (4 + 2 * k, 5 + 2 * k) if k < 2 else ()
             if k >= 1:
                 transpose_attn(k - 1)
@@ -259,18 +283,19 @@ def tile_crossxmfusion_pa_kernel(tc, feature_x, feature_m, out_0, out_1):
                 product("m", k - 2)
             if k + 2 < TILES:
                 quantise_x_t(k + 2)
+            if k + 2 < TILES:
                 logits(k + 2)
-            share = VECTOR_SHARE if k >= 2 else HALF
-            regroup(nc.vector.tensor_copy, k + 2, 0, share)
+            share = (320, 384)[k] if k < 2 else 96
+            if share:
+                regroup(V, k + 2, 0, share)
+            share = (320, 384)[k] if k < 2 else 96
             if share < HALF:
-                regroup(nc.scalar.copy, k + 2, share, HALF)
+                regroup(S, k + 2, share, HALF)
             if k >= 1:
                 copy_attn_d(k - 1)
             for i in late_x:
                 copy_x_t(i)
-            reciprocal(k)
-            nc.gpsimd.tensor_scalar(out=attn_sb[k // 4][:, k % 4, :], in0=exp_sb[k][:], scalar1=inv_sum[k][:],
-                                    scalar2=0.0, op0=ALU.mult, op1=ALU.add)
+            normalise(k)
             row_max(k + 1)
             if k >= 2:
                 add_residual("m", k - 2, 0)
@@ -280,59 +305,78 @@ def tile_crossxmfusion_pa_kernel(tc, feature_x, feature_m, out_0, out_1):
                 add_residual("m", k - 2, 1)
                 store("m", k - 2)
 
-        last = TILES - 1
+        transpose_attn(5)
+        copy_attn_d(5)
+        quantise_attn_d(4)
+        quantise_chunk(7)
+        regroup(V, 8, 0, PIECE)
+        regroup(S, 8, PIECE, HALF)
+        product("m", 4)
+        row_max(7)
+        row_shift(7)
+        quantise_attn_d(5)
+        product("m", 5)
+        normalise(6)
+        exponentials(7)
+        add_residual("m", 4, 0)
+        add_residual("m", 4, 1)
+        store("m", 4)
+        regroup(S, 9, 0, PIECE)
 
-        def regroup_piece(copy, q, lo=0, hi=PIECE):
-            regroup(copy, 10 + q // 2, PIECE * (q % 2) + lo, PIECE * (q % 2) + hi)
+        def regroup_piece(copy, q):
+            regroup(copy, 10 + q // 2, PIECE * (q % 2), PIECE * (q % 2 + 1))
 
         def quantise_piece(q):
             quantise_chunk(10 + q // 2, PIECE * (q % 2), PIECE * (q % 2 + 1))
 
-        jobs = []
-        for n in range(3):
-            jobs += [("m", last - 2 + n), ("x", 2 * n), ("x", 2 * n + 1)]
-        jobs += [("x", 6), ("x", 7)]
-
-        transpose_attn(last - 1)
-        quantise_attn_d(last - 2)
-        quantise_chunk(8)
-        product("m", last - 2)
-        product("x", 0, (0,))
-        product("x", 1, (0,))
-        copy_attn_d(last - 1)
-        reciprocal(last)
-        nc.vector.tensor_scalar(out=attn_sb[last // 4][:, last % 4, :], in0=exp_sb[last][:], scalar1=inv_sum[last][:],
-                                scalar2=None, op0=ALU.mult)
-        transpose_attn(last)
-        regroup_piece(nc.vector.tensor_copy, 0)
-        regroup_piece(nc.vector.tensor_copy, 1)
-        regroup(nc.scalar.copy, 9, 0, HALF)
-        copy_attn_d(last)
-        regroup_piece(nc.scalar.copy, 2)
-        regroup_piece(nc.scalar.copy, 3)
-
-        def prepare(name, i):
-            if name == "m":
-                quantise_attn_d(i)
-            elif i % 2 == 0:
-                if i == 4:
-                    quantise_chunk(9)
-                quantise_piece(i // 2)
-
-        prepare("x", 0)
-        product("x", 0, (1,))
-        product("x", 1, (1,))
-        prepare("m", last - 1)
-        prepare("x", 2)
-        for n, (name, i) in enumerate(jobs):
-            halves = n == 1 or n == len(jobs) - 1
+        def finish(name, i, by_gpsimd=(), halves=False):
             for h in range(2):
-                add_residual(name, i, h, by_gpsimd=(h == 1 and 4 <= n <= 8))
+                add_residual(name, i, h, by_gpsimd=h in by_gpsimd)
                 if halves:
                     store(name, i, h * HALF, (h + 1) * HALF)
             if not halves:
                 store(name, i)
-            if n + 5 < len(jobs):
-                prepare(jobs[n + 5][0], jobs[n + 5][1])
-            if n + 3 < len(jobs):
-                product(jobs[n + 3][0], jobs[n + 3][1])
+
+        transpose_attn(6)
+        quantise_chunk(8)
+        reciprocal(7)
+        nc.vector.tensor_scalar(out=attn_sb[1][:, 3, :], in0=exp_sb[7][:], scalar1=inv_sum[7][:],
+                                scalar2=None, op0=ALU.mult)
+        product("x", 0, (0,))
+        product("x", 1, (0,))
+        transpose_attn(7)
+        copy_attn_d(6)
+        regroup_piece(V, 0)
+        regroup_piece(S, 1)
+        copy_attn_d(7)
+        quantise_piece(0)
+        finish("m", 5)
+        product("x", 0, (1,))
+        quantise_attn_d(6)
+        product("m", 6)
+        finish("x", 0)
+        quantise_piece(1)
+        product("x", 1, (1,))
+        regroup_piece(S, 2)
+        regroup_piece(S, 3)
+        regroup(S, 9, PIECE, HALF)
+        finish("m", 6)
+        quantise_attn_d(7)
+        product("x", 2)
+        finish("x", 1)
+        quantise_piece(2)
+        product("x", 3)
+        quantise_piece(3)
+        product("m", 7)
+        finish("x", 2)
+        quantise_chunk(9)
+        finish("x", 3)
+        product("x", 4)
+        finish("m", 7)
+        product("x", 5)
+        finish("x", 4)
+        product("x", 6)
+        finish("x", 5)
+        product("x", 7)
+        finish("x", 6)
+        finish("x", 7, halves=True)

@@ -42,6 +42,8 @@ def tile_crossxmfusion_pa_kernel(tc, feature_x, feature_m, out_0, out_1):
         nc.vector.memset(warm[:, 0:1], 0.0)
         nc.scalar.activation(out=warm[:, 1:2], in_=warm[:, 0:1], func=ACT.Exp)
 
+        zeros = keep.tile([P, HALF], BF16, name="zeros")
+        nc.gpsimd.memset(zeros[:], 0.0)
         ident_f32 = keep.tile([P, P], F32, name="ident_f32")
         make_identity(nc, ident_f32[:])
 
@@ -92,6 +94,9 @@ def tile_crossxmfusion_pa_kernel(tc, feature_x, feature_m, out_0, out_1):
         def bank(shape, dtype):
             return psum.tile(shape, dtype, name="bank")
 
+        def idle_matmul(bank_tile):
+            nc.tensor.matmul(bank_tile, lhsT=zeros[:, 0:P], rhs=zeros[:], start=True, stop=True)
+
         words_ps = {}
         x_t_grouped = {}
         m_t_grouped = {}
@@ -99,6 +104,8 @@ def tile_crossxmfusion_pa_kernel(tc, feature_x, feature_m, out_0, out_1):
         def transpose_words(key, sb, i):
             words = sb[i // 4][:, i % 4, :].bitcast(F32)
             ps = bank([P, 4, P], F32)
+            for n in range(3 if i == 1 else 0):
+                idle_matmul(ps[:].rearrange("p b c -> p (b c)"))
             for b in range(4):
                 nc.tensor.transpose(ps[:, b, :], words[:, P * b : P * (b + 1)], ident_f32[:])
             words_ps[key, i] = ps[:].rearrange("p (s u) c -> p s c u", s=2, u=2)
@@ -113,6 +120,9 @@ def tile_crossxmfusion_pa_kernel(tc, feature_x, feature_m, out_0, out_1):
 
         def transpose_m_words(g, u, s):
             ps = bank([P, 2, 2, P], F32)
+            if s == 0:
+                for n in range(8 if (g, u) == (0, 0) else 1):
+                    idle_matmul(ps[:].rearrange("p e v c -> p (e v c)"))
             for e in range(2):
                 words = m_sb[g][:, 2 * u + e, :].bitcast(F32)
                 for v in range(2):
@@ -198,6 +208,7 @@ def tile_crossxmfusion_pa_kernel(tc, feature_x, feature_m, out_0, out_1):
         def transpose_attn(i):
             words = attn_sb[i // 4][:, i % 4, :].bitcast(F32)
             ps = bank([P, 4, P], F32)
+            idle_matmul(ps[:].rearrange("p b c -> p (b c)"))
             for b in range(4):
                 nc.tensor.transpose(ps[:, b, :], words[:, P * b : P * (b + 1)], ident_f32[:])
             attn_t_ps[i] = ps[:].rearrange("p (s u) c -> p s c u", s=2, u=2)

@@ -43,7 +43,7 @@ def tile_crossxmfusion_pa_kernel(tc, feature_x, feature_m, out_0, out_1):
         nc.scalar.activation(out=warm[:, 1:2], in_=warm[:, 0:1], func=ACT.Exp)
 
         zeros = keep.tile([P, HALF], BF16, name="zeros")
-        nc.gpsimd.memset(zeros[:], 0.0)
+        nc.vector.memset(zeros[:], 0.0)
         ident_f32 = keep.tile([P, P], F32, name="ident_f32")
         make_identity(nc, ident_f32[:])
 
@@ -51,12 +51,14 @@ def tile_crossxmfusion_pa_kernel(tc, feature_x, feature_m, out_0, out_1):
         m_sb = [keep.tile([P, 4, N], BF16, name="m_sb%d" % g, align_bytes=64) for g in range(2)]
         attn_sb = [keep.tile([P, 4, N], BF16, name="attn_sb%d" % g, align_bytes=64) for g in range(2)]
 
-        def load(sb, dram, g, j0, j1):
-            nc.sync.dma_start(out=sb[g][:, j0:j1, :], in_=dram[:, g, j0:j1, :])
+        def load(sb, dram, g, j0, j1, lo=0, hi=N):
+            nc.sync.dma_start(out=sb[g][:, j0:j1, lo:hi], in_=dram[:, g, j0:j1, lo:hi])
 
-        for g in range(2):
-            load(m_sb, m_dram, g, 0, 2)
-            load(m_sb, m_dram, g, 2, 4)
+        load(m_sb, m_dram, 0, 0, 2, 0, HALF)
+        load(m_sb, m_dram, 0, 0, 2, HALF, N)
+        load(m_sb, m_dram, 0, 2, 4)
+        load(m_sb, m_dram, 1, 0, 2)
+        load(m_sb, m_dram, 1, 2, 4)
         load(x_sb, x_dram, 0, 0, 1)
         load(x_sb, x_dram, 0, 1, 4)
         load(x_sb, x_dram, 1, 0, 2)
@@ -121,7 +123,7 @@ def tile_crossxmfusion_pa_kernel(tc, feature_x, feature_m, out_0, out_1):
         def transpose_m_words(g, u, s):
             ps = bank([P, 2, 2, P], F32)
             if s == 0:
-                for n in range(8 if (g, u) == (0, 0) else 1):
+                for n in range(4 if (g, u) == (0, 0) else 1):
                     idle_matmul(ps[:].rearrange("p e v c -> p (e v c)"))
             for e in range(2):
                 words = m_sb[g][:, 2 * u + e, :].bitcast(F32)
@@ -170,6 +172,7 @@ def tile_crossxmfusion_pa_kernel(tc, feature_x, feature_m, out_0, out_1):
         shift = {}
         exp_sb = {}
         half_sum = {}
+        row_sum = {}
         inv_sum = {}
 
         def logits(i):
@@ -195,12 +198,14 @@ def tile_crossxmfusion_pa_kernel(tc, feature_x, feature_m, out_0, out_1):
                 nc.scalar.activation(out=exp_sb[i][:, h * HALF : (h + 1) * HALF], in_=logits_ps[i][h][:], func=ACT.Exp,
                                      bias=shift[i][:], scale=1.0 / N, accum_out=half_sum[i][:, h : h + 1])
 
-        def reciprocal(i):
-            row_sum = small.tile([P, 1], F32, name="row_sum")
-            nc.vector.tensor_scalar(out=row_sum[:], in0=half_sum[i][:, 0:1], scalar1=half_sum[i][:, 1:2],
+        def row_total(i):
+            row_sum[i] = small.tile([P, 1], F32, name="row_sum")
+            nc.vector.tensor_scalar(out=row_sum[i][:], in0=half_sum[i][:, 0:1], scalar1=half_sum[i][:, 1:2],
                                     scalar2=None, op0=ALU.add)
+
+        def reciprocal(i):
             inv_sum[i] = small.tile([P, 1], F32, name="inv_sum")
-            nc.vector.reciprocal(out=inv_sum[i][:], in_=row_sum[:])
+            nc.vector.reciprocal(out=inv_sum[i][:], in_=row_sum[i][:])
 
         attn_t_ps = {}
         attn_d_grouped = {}
@@ -265,10 +270,12 @@ def tile_crossxmfusion_pa_kernel(tc, feature_x, feature_m, out_0, out_1):
             for s in range(2):
                 quantise_m_t(g, u, s)
             if q in (1, 2):
-                regroup(nc.vector.tensor_copy, 0, PIECE * (q // 2), PIECE * (q // 2 + 1))
+                regroup(nc.vector.tensor_copy, 0, PIECE * (q // 2), PIECE * (q // 2 + 1) - (P if q == 2 else 0))
         for i in range(4):
             transpose_words("x", x_sb, i)
             copy_x_t(i)
+            if i == 0:
+                regroup(nc.scalar.copy, 0, HALF - P, HALF)
             if i < 2:
                 quantise_x_t(i)
             if i == 0:
@@ -296,6 +303,8 @@ def tile_crossxmfusion_pa_kernel(tc, feature_x, feature_m, out_0, out_1):
                 quantise_x_t(k + 2)
             if k + 2 < TILES:
                 logits(k + 2)
+            if k >= 2:
+                row_total(k)
             share = (320, 384)[k] if k < 2 else 96
             if share:
                 regroup(V, k + 2, 0, share)
@@ -306,6 +315,8 @@ def tile_crossxmfusion_pa_kernel(tc, feature_x, feature_m, out_0, out_1):
                 copy_attn_d(k - 1)
             for i in late_x:
                 copy_x_t(i)
+            if k < 2:
+                row_total(k)
             normalise(k)
             row_max(k + 1)
             if k >= 2:
@@ -327,6 +338,7 @@ def tile_crossxmfusion_pa_kernel(tc, feature_x, feature_m, out_0, out_1):
         row_shift(7)
         quantise_attn_d(5)
         product("m", 5)
+        row_total(6)
         normalise(6)
         exponentials(7)
         add_residual("m", 4, 0)
@@ -349,6 +361,7 @@ def tile_crossxmfusion_pa_kernel(tc, feature_x, feature_m, out_0, out_1):
                 store(name, i)
 
         transpose_attn(6)
+        row_total(7)
         quantise_chunk(8)
         reciprocal(7)
         nc.vector.tensor_scalar(out=attn_sb[1][:, 3, :], in0=exp_sb[7][:], scalar1=inv_sum[7][:],

@@ -327,30 +327,23 @@ def tile_crossxmfusion_pa_kernel(tc, feature_x, feature_m, out_0, out_1):
                 add_residual("m", k - 2, 1)
                 store("m", k - 2)
 
-        transpose_attn(5)
-        copy_attn_d(5)
-        quantise_attn_d(4)
-        quantise_chunk(7)
-        regroup(V, 8, 0, PIECE)
-        regroup(S, 8, PIECE, HALF)
-        product("m", 4)
-        row_max(7)
-        row_shift(7)
-        quantise_attn_d(5)
-        product("m", 5)
-        row_total(6)
-        normalise(6)
-        exponentials(7)
-        add_residual("m", 4, 0)
-        add_residual("m", 4, 1)
-        store("m", 4)
-        regroup(S, 9, 0, PIECE)
+        piece_grouped = {}
 
-        def regroup_piece(copy, q):
-            regroup(copy, 10 + q // 2, PIECE * (q % 2), PIECE * (q % 2 + 1))
+        def piece_columns(n, q):
+            name, g, h = chunks[n]
+            start = h * HALF + q * PIECE
+            return attn_sb[g][:, :, start : start + PIECE].rearrange("p j (c e) -> p e c j", e=2)
 
-        def quantise_piece(q):
-            quantise_chunk(10 + q // 2, PIECE * (q % 2), PIECE * (q % 2 + 1))
+        def regroup_piece(copy, n, q, tag):
+            piece_grouped[n, q] = stage.tile([P, PIECE, 4], BF16, name=tag, bufs=1, align_bytes=64)
+            copy(out=piece_grouped[n, q][:].rearrange("p (e c) j -> p e c j", e=2), in_=piece_columns(n, q))
+
+        def G(out, in_):
+            nc.gpsimd.tensor_scalar(out=out, in0=in_, scalar1=1.0, scalar2=0.0, op0=ALU.mult, op1=ALU.add)
+
+        def quantise_piece(n, q):
+            name, g, h = chunks[n]
+            quantise(by_channel[name], g * N + h * HALF + q * PIECE, piece_grouped[n, q][:].rearrange("p c j -> p (c j)"))
 
         def finish(name, i, by_gpsimd=(), halves=False):
             for h in range(2):
@@ -360,43 +353,61 @@ def tile_crossxmfusion_pa_kernel(tc, feature_x, feature_m, out_0, out_1):
             if not halves:
                 store(name, i)
 
+        transpose_attn(5)
+        quantise_attn_d(4)
+        product("m", 4)
+        row_max(7)
+        row_shift(7)
+        copy_attn_d(5)
+        exponentials(7)
+        row_total(6)
+        normalise(6)
+        finish("m", 4)
         transpose_attn(6)
+        quantise_attn_d(5)
+        product("m", 5)
+        regroup_piece(S, 8, 0, "p80")
         row_total(7)
-        quantise_chunk(8)
         reciprocal(7)
-        nc.vector.tensor_scalar(out=attn_sb[1][:, 3, :], in0=exp_sb[7][:], scalar1=inv_sum[7][:],
-                                scalar2=None, op0=ALU.mult)
-        product("x", 0, (0,))
-        product("x", 1, (0,))
-        transpose_attn(7)
+        nc.vector.tensor_scalar(out=attn_sb[1][:, 3, :], in0=exp_sb[7][:], scalar1=inv_sum[7][:], scalar2=None, op0=ALU.mult)
         copy_attn_d(6)
-        regroup_piece(V, 0)
-        regroup_piece(S, 1)
-        copy_attn_d(7)
-        quantise_piece(0)
-        finish("m", 5)
-        product("x", 0, (1,))
+        quantise_chunk(7)
+        transpose_attn(7)
+        regroup_piece(V, 10, 0, "gate0")
+        quantise_piece(8, 0)
         quantise_attn_d(6)
+        product("x", 0, (0,))
+        quantise_piece(10, 0)
+        regroup_piece(G, 9, 0, "gate0")
+        product("x", 0, (1,))
         product("m", 6)
+        regroup_piece(S, 10, 1, "gate1")
+        copy_attn_d(7)
+        regroup_piece(S, 8, 1, "p81")
+        finish("m", 5)
+        product("x", 1)
         finish("x", 0)
-        quantise_piece(1)
-        product("x", 1, (1,))
-        regroup_piece(S, 2)
-        regroup_piece(S, 3)
-        regroup(S, 9, PIECE, HALF)
         finish("m", 6)
         quantise_attn_d(7)
+        quantise_piece(8, 1)
+        quantise_piece(9, 0)
+        quantise_piece(10, 1)
+        regroup_piece(G, 9, 1, "gate1")
+        product("m", 7)
         product("x", 2)
         finish("x", 1)
-        quantise_piece(2)
+        regroup_piece(S, 11, 0, "p110")
+        regroup_piece(S, 11, 1, "p111")
+        add_residual("m", 7, 0)
+        add_residual("m", 7, 1, True)
+        store("m", 7)
         product("x", 3)
-        quantise_piece(3)
-        product("m", 7)
         finish("x", 2)
-        quantise_chunk(9)
-        finish("x", 3)
+        quantise_piece(11, 0)
+        quantise_piece(11, 1)
+        quantise_piece(9, 1)
         product("x", 4)
-        finish("m", 7)
+        finish("x", 3)
         product("x", 5)
         finish("x", 4)
         product("x", 6)

@@ -64,25 +64,49 @@ def tile_crossxmfusion_pa_kernel(tc, feature_x, feature_m, out_0, out_1):
         load(x_sb, x_dram, 1, 0, 2)
         load(x_sb, x_dram, 1, 2, 4)
 
-        def operand(name):
+        def operand(name, words):
             return (
-                keep.tile([P, 2 * N], U32, name=name + "_codes", align_bytes=64),
-                keep.tile([P, 2 * N], U8, name=name + "_scales", align_bytes=64),
+                keep.tile([P, words], U32, name=name + "_codes", align_bytes=64),
+                keep.tile([P, words], U8, name=name + "_scales", align_bytes=64),
             )
 
-        x_t = operand("x_t")
-        m_t = operand("m_t")
-        attn_d = operand("attn_d")
-        by_channel = {"m": operand("m_c"), "x": operand("x_c"), "attn": operand("attn_c")}
+        m_t = operand("m_t", 2 * N)
+        x_t_first = operand("x_t_first", N)
+        attn_d_last = operand("attn_d_last", N)
+        by_channel = [operand("chunk%d" % n, HALF) if n not in (3, 4, 5, 6) else None for n in range(8)]
+        attn_c = [operand("attn_c%d" % b, HALF) for b in range(4)]
+        by_step = {k: operand("step%d" % k, N) for k in range(2, 6)}
+
+        def place_of_x_t(i):
+            return (by_step[i - 2], PIECE) if i >= 4 else (x_t_first, PIECE * i)
+
+        def place_of_attn_d(i):
+            return (by_step[i + 2], 0) if i < 4 else (attn_d_last, PIECE * (i - 4))
+
+        def place_of_chunk(n):
+            return (by_step[n - 1], HALF) if 3 <= n <= 6 else (by_channel[n], 0)
+
         plain = {"m": m_sb, "x": x_sb, "attn": attn_sb}
+
+        step_grouped = {}
+
+        def group_of_step(k):
+            if k not in step_grouped:
+                step_grouped[k] = stage.tile([P, 4 * N], BF16, name="step_grouped", bufs=4, align_bytes=64)
+            return step_grouped[k]
+
+        def quantise_step(k):
+            quantise(by_step[k], 0, step_grouped[k][:])
 
         def quantise(dst, start, grouped):
             words = slice(start, start + grouped.shape[1] // 4)
             nc.vector.quantize_mx(out=dst[0][:, words].bitcast(FP8X4), scales=dst[1][:, words], in_=grouped)
 
-        def mx_pass(acc, a, a_start, b, b_start, s):
-            a_cols = slice(a_start, a_start + P)
-            b_cols = slice(b_start, b_start + HALF)
+        def mx_pass(acc, a_place, a_offset, b_place, b_offset, s):
+            a, a_start = a_place
+            b, b_start = b_place
+            a_cols = slice(a_start + a_offset, a_start + a_offset + P)
+            b_cols = slice(b_start + b_offset, b_start + b_offset + HALF)
             nc.tensor.matmul_mx(
                 out=acc,
                 lhsT=a[0][:, a_cols].bitcast(FP8X4),
@@ -113,12 +137,16 @@ def tile_crossxmfusion_pa_kernel(tc, feature_x, feature_m, out_0, out_1):
             words_ps[key, i] = ps[:].rearrange("p (s u) c -> p s c u", s=2, u=2)
 
         def copy_x_t(i):
-            x_t_grouped[i] = stage.tile([P, N], BF16, name="x_t_grouped", bufs=6, align_bytes=64)
-            nc.scalar.copy(out=x_t_grouped[i][:].bitcast(F32).rearrange("p (s c u) -> p s c u", s=2, u=2),
+            if i >= 4:
+                grouped = group_of_step(i - 2)[:, N : 2 * N]
+            else:
+                x_t_grouped[i] = stage.tile([P, N], BF16, name="x_t_grouped", bufs=4, align_bytes=64)
+                grouped = x_t_grouped[i][:]
+            nc.scalar.copy(out=grouped.bitcast(F32).rearrange("p (s c u) -> p s c u", s=2, u=2),
                            in_=words_ps["x", i])
 
         def quantise_x_t(i):
-            quantise(x_t, 2 * P * i, x_t_grouped[i][:])
+            quantise(x_t_first, PIECE * i, x_t_grouped[i][:])
 
         def transpose_m_words(g, u, s):
             ps = bank([P, 2, 2, P], F32)
@@ -133,7 +161,7 @@ def tile_crossxmfusion_pa_kernel(tc, feature_x, feature_m, out_0, out_1):
             words_ps["m", g, u, s] = ps[:].rearrange("p e v c -> p c e v")
 
         def copy_m_t(copy, g, u, s):
-            m_t_grouped[g, u, s] = stage.tile([P, N], BF16, name="m_t_grouped", bufs=8, align_bytes=64)
+            m_t_grouped[g, u, s] = stage.tile([P, N], BF16, name="m_t_grouped", bufs=6, align_bytes=64)
             copy(out=m_t_grouped[g, u, s][:].bitcast(F32).rearrange("p (c e v) -> p c e v", e=2, v=2),
                  in_=words_ps["m", g, u, s])
 
@@ -148,7 +176,10 @@ def tile_crossxmfusion_pa_kernel(tc, feature_x, feature_m, out_0, out_1):
         def regroup(copy, n, lo, hi):
             name, g, h = chunks[n]
             if n not in chunk_grouped:
-                chunk_grouped[n] = stage.tile([P, HALF, 4], BF16, name="chunk_grouped", bufs=5, align_bytes=64)
+                if 3 <= n <= 6:
+                    chunk_grouped[n] = group_of_step(n - 1)[:, 2 * N :].rearrange("p (c j) -> p c j", j=4)
+                else:
+                    chunk_grouped[n] = stage.tile([P, HALF, 4], BF16, name="chunk_grouped", bufs=3, align_bytes=64)
             if name == "attn":
                 for c0 in range(lo, hi, P):
                     u, e = divmod(c0 // P, 2)
@@ -164,7 +195,7 @@ def tile_crossxmfusion_pa_kernel(tc, feature_x, feature_m, out_0, out_1):
 
         def quantise_chunk(n, lo=0, hi=HALF):
             name, g, h = chunks[n]
-            quantise(by_channel[name], g * N + h * HALF + lo,
+            quantise(by_channel[n], lo,
                      chunk_grouped[n][:, lo:hi, :].rearrange("p c j -> p (c j)"))
 
         logits_ps = {}
@@ -179,7 +210,7 @@ def tile_crossxmfusion_pa_kernel(tc, feature_x, feature_m, out_0, out_1):
             logits_ps[i] = [bank([P, HALF], F32) for h in range(2)]
             for h in range(2):
                 for s in range(2):
-                    mx_pass(logits_ps[i][h][:], x_t, 2 * P * i + s * P, m_t, s * N + h * HALF, s)
+                    mx_pass(logits_ps[i][h][:], place_of_x_t(i), s * P, (m_t, s * N + h * HALF), 0, s)
 
         def row_max(i):
             half_max[i] = small.tile([P, 2], F32, name="half_max")
@@ -213,18 +244,23 @@ def tile_crossxmfusion_pa_kernel(tc, feature_x, feature_m, out_0, out_1):
         def transpose_attn(i):
             words = attn_sb[i // 4][:, i % 4, :].bitcast(F32)
             ps = bank([P, 4, P], F32)
-            idle_matmul(ps[:].rearrange("p b c -> p (b c)"))
+            for n in range(4 if i in (0, 6) else 1):
+                idle_matmul(ps[:].rearrange("p b c -> p (b c)"))
             for b in range(4):
                 nc.tensor.transpose(ps[:, b, :], words[:, P * b : P * (b + 1)], ident_f32[:])
             attn_t_ps[i] = ps[:].rearrange("p (s u) c -> p s c u", s=2, u=2)
 
         def copy_attn_d(i):
-            attn_d_grouped[i] = stage.tile([P, N], BF16, name="attn_d_grouped", bufs=3, align_bytes=64)
-            nc.scalar.copy(out=attn_d_grouped[i][:].bitcast(F32).rearrange("p (s c u) -> p s c u", s=2, u=2),
+            if i < 4:
+                grouped = group_of_step(i + 2)[:, 0:N]
+            else:
+                attn_d_grouped[i] = stage.tile([P, N], BF16, name="attn_d_grouped", bufs=3, align_bytes=64)
+                grouped = attn_d_grouped[i][:]
+            nc.scalar.copy(out=grouped.bitcast(F32).rearrange("p (s c u) -> p s c u", s=2, u=2),
                            in_=attn_t_ps[i])
 
         def quantise_attn_d(i):
-            quantise(attn_d, 2 * P * i, attn_d_grouped[i][:])
+            quantise(attn_d_last, PIECE * (i - 4), attn_d_grouped[i][:])
 
         acc_ps = {}
         result = {}
@@ -235,13 +271,13 @@ def tile_crossxmfusion_pa_kernel(tc, feature_x, feature_m, out_0, out_1):
                     acc_ps[name, i, h] = bank([P, HALF], F32)
                 for s in passes:
                     if name == "m":
-                        mx_pass(acc_ps[name, i, h][:], attn_d, 2 * P * i + s * P, by_channel["m"], s * N + h * HALF, s)
+                        mx_pass(acc_ps[name, i, h][:], place_of_attn_d(i), s * P, place_of_chunk(2 * s + h), 0, s)
                     else:
-                        mx_pass(acc_ps[name, i, h][:], by_channel["attn"], s * N + i * P, by_channel["x"], s * N + h * HALF, s)
+                        mx_pass(acc_ps[name, i, h][:], (attn_c[i // 2], PIECE * s), i % 2 * P, place_of_chunk(4 + 2 * s + h), 0, s)
 
         def add_residual(name, i, h, by_gpsimd=False):
             if h == 0:
-                result[name, i] = stage.tile([P, N], F32, name="result", bufs=12)
+                result[name, i] = stage.tile([P, N], F32, name="result", bufs=8)
             cols = slice(h * HALF, (h + 1) * HALF)
             out = result[name, i][:, cols]
             residual = plain[name][i // 4][:, i % 4, cols]
@@ -295,14 +331,12 @@ def tile_crossxmfusion_pa_kernel(tc, feature_x, feature_m, out_0, out_1):
             for i in late_x:
                 transpose_words("x", x_sb, i)
             if k >= 2:
-                quantise_attn_d(k - 2)
-            quantise_chunk(k + 1)
-            if k >= 2:
+                quantise_step(k)
                 product("m", k - 2)
-            if k + 2 < TILES:
+            else:
+                quantise_chunk(k + 1)
                 quantise_x_t(k + 2)
-            if k + 2 < TILES:
-                logits(k + 2)
+            logits(k + 2)
             if k >= 2:
                 row_total(k)
             share = (320, 384)[k] if k < 2 else 96
@@ -327,27 +361,24 @@ def tile_crossxmfusion_pa_kernel(tc, feature_x, feature_m, out_0, out_1):
                 add_residual("m", k - 2, 1)
                 store("m", k - 2)
 
-        piece_grouped = {}
+        pair_grouped = {}
 
-        def piece_columns(n, q):
-            name, g, h = chunks[n]
-            start = h * HALF + q * PIECE
-            return attn_sb[g][:, :, start : start + PIECE].rearrange("p j (c e) -> p e c j", e=2)
-
-        def regroup_piece(copy, n, q, tag):
-            piece_grouped[n, q] = stage.tile([P, PIECE, 4], BF16, name=tag, bufs=1, align_bytes=64)
-            copy(out=piece_grouped[n, q][:].rearrange("p (e c) j -> p e c j", e=2), in_=piece_columns(n, q))
+        def regroup_pair(copy, b, g):
+            if b not in pair_grouped:
+                pair_grouped[b] = stage.tile([P, 2, PIECE, 4], BF16, name="pair_grouped%d" % (b % 2), bufs=1, align_bytes=64)
+            copy(out=pair_grouped[b][:, g, :, :].rearrange("p (e c) j -> p e c j", e=2),
+                 in_=attn_sb[g][:, :, PIECE * b : PIECE * (b + 1)].rearrange("p j (c e) -> p e c j", e=2))
 
         def G(out, in_):
             nc.gpsimd.tensor_scalar(out=out, in0=in_, scalar1=1.0, scalar2=0.0, op0=ALU.mult, op1=ALU.add)
 
-        def quantise_piece(n, q):
-            name, g, h = chunks[n]
-            quantise(by_channel[name], g * N + h * HALF + q * PIECE, piece_grouped[n, q][:].rearrange("p c j -> p (c j)"))
+        def quantise_pair(b, parts=(0, 1)):
+            first, last = parts[0], parts[-1]
+            quantise(attn_c[b], PIECE * first, pair_grouped[b][:, first : last + 1, :, :].rearrange("p g c j -> p (g c j)"))
 
-        def finish(name, i, by_gpsimd=(), halves=False):
+        def finish(name, i, halves=False):
             for h in range(2):
-                add_residual(name, i, h, by_gpsimd=h in by_gpsimd)
+                add_residual(name, i, h)
                 if halves:
                     store(name, i, h * HALF, (h + 1) * HALF)
             if not halves:
@@ -366,46 +397,41 @@ def tile_crossxmfusion_pa_kernel(tc, feature_x, feature_m, out_0, out_1):
         transpose_attn(6)
         quantise_attn_d(5)
         product("m", 5)
-        regroup_piece(S, 8, 0, "p80")
+        regroup_pair(S, 0, 0)
         row_total(7)
         reciprocal(7)
         nc.vector.tensor_scalar(out=attn_sb[1][:, 3, :], in0=exp_sb[7][:], scalar1=inv_sum[7][:], scalar2=None, op0=ALU.mult)
         copy_attn_d(6)
         quantise_chunk(7)
         transpose_attn(7)
-        regroup_piece(V, 10, 0, "gate0")
-        quantise_piece(8, 0)
+        regroup_pair(S, 0, 1)
+        quantise_pair(0, (0,))
         quantise_attn_d(6)
-        product("x", 0, (0,))
-        quantise_piece(10, 0)
-        regroup_piece(G, 9, 0, "gate0")
-        product("x", 0, (1,))
-        product("m", 6)
-        regroup_piece(S, 10, 1, "gate1")
-        copy_attn_d(7)
-        regroup_piece(S, 8, 1, "p81")
         finish("m", 5)
+        product("m", 6)
+        product("x", 0, (0,))
+        quantise_pair(0, (1,))
+        regroup_pair(G, 2, 1)
+        product("x", 0, (1,))
+        copy_attn_d(7)
+        regroup_pair(S, 1, 1)
+        regroup_pair(S, 1, 0)
+        finish("m", 6)
         product("x", 1)
         finish("x", 0)
-        finish("m", 6)
         quantise_attn_d(7)
-        quantise_piece(8, 1)
-        quantise_piece(9, 0)
-        quantise_piece(10, 1)
-        regroup_piece(G, 9, 1, "gate1")
+        quantise_pair(1)
+        regroup_pair(G, 3, 0)
         product("m", 7)
         product("x", 2)
         finish("x", 1)
-        regroup_piece(S, 11, 0, "p110")
-        regroup_piece(S, 11, 1, "p111")
-        add_residual("m", 7, 0)
-        add_residual("m", 7, 1, True)
-        store("m", 7)
+        regroup_pair(S, 2, 0)
+        regroup_pair(S, 3, 1)
+        finish("m", 7)
         product("x", 3)
         finish("x", 2)
-        quantise_piece(11, 0)
-        quantise_piece(11, 1)
-        quantise_piece(9, 1)
+        quantise_pair(2)
+        quantise_pair(3)
         product("x", 4)
         finish("x", 3)
         product("x", 5)

@@ -275,17 +275,13 @@ def tile_crossxmfusion_pa_kernel(tc, feature_x, feature_m, out_0, out_1):
                     else:
                         mx_pass(acc_ps[name, i, h][:], (attn_c[i // 2], PIECE * s), i % 2 * P, place_of_chunk(4 + 2 * s + h), 0, s)
 
-        def add_residual(name, i, h, by_gpsimd=False):
+        def add_residual(name, i, h):
             if h == 0:
                 result[name, i] = stage.tile([P, N], F32, name="result", bufs=8)
             cols = slice(h * HALF, (h + 1) * HALF)
             out = result[name, i][:, cols]
             residual = plain[name][i // 4][:, i % 4, cols]
-            if by_gpsimd:
-                nc.scalar.copy(out=out, in_=acc_ps[name, i, h][:])
-                nc.gpsimd.tensor_tensor(out=out, in0=out, in1=residual, op=ALU.add)
-            else:
-                nc.vector.tensor_tensor(out=out, in0=acc_ps[name, i, h][:], in1=residual, op=ALU.add)
+            nc.vector.tensor_tensor(out=out, in0=acc_ps[name, i, h][:], in1=residual, op=ALU.add)
 
         def store(name, i, lo=0, hi=N):
             nc.sync.dma_start(out=out_dram[name][:, i // 4, i % 4, lo:hi], in_=result[name, i][:, lo:hi])
@@ -376,12 +372,12 @@ def tile_crossxmfusion_pa_kernel(tc, feature_x, feature_m, out_0, out_1):
             first, last = parts[0], parts[-1]
             quantise(attn_c[b], PIECE * first, pair_grouped[b][:, first : last + 1, :, :].rearrange("p g c j -> p (g c j)"))
 
-        def finish(name, i, halves=False):
+        def finish(name, i, parts=1):
             for h in range(2):
                 add_residual(name, i, h)
-                if halves:
+                if parts == 2:
                     store(name, i, h * HALF, (h + 1) * HALF)
-            if not halves:
+            if parts == 1:
                 store(name, i)
 
         transpose_attn(5)
@@ -431,13 +427,13 @@ def tile_crossxmfusion_pa_kernel(tc, feature_x, feature_m, out_0, out_1):
         product("x", 3)
         finish("x", 2)
         quantise_pair(2)
-        quantise_pair(3)
         product("x", 4)
-        finish("x", 3)
+        finish("x", 3, parts=2)
+        quantise_pair(3)
         product("x", 5)
-        finish("x", 4)
+        finish("x", 4, parts=2)
         product("x", 6)
-        finish("x", 5)
+        finish("x", 5, parts=2)
         product("x", 7)
-        finish("x", 6)
-        finish("x", 7, halves=True)
+        finish("x", 6, parts=2)
+        finish("x", 7, parts=2)

from contextlib import ExitStack

import concourse.mybir as mybir
from concourse.masks import make_identity

FLOPS = 3 * 2 * 1024 * 1024 * 1024

F32 = mybir.dt.float32
BF16 = mybir.dt.bfloat16
U32 = mybir.dt.uint32
U8 = mybir.dt.uint8
FP8X4 = mybir.dt.float8_e4m3fn_x4
ALU = mybir.AluOpType
ACT = mybir.ActivationFunctionType
AX = mybir.AxisListType

P = 128
N = 1024
HALF = 512
TILES = 8
PIECE = 256


def tile_crossxmfusion_pa_kernel(tc, feature_x, feature_m, out_0, out_1):
    nc = tc.nc
    by_tile = "(g p j) t -> p g j t"
    x_dram = feature_x.flatten_outer_dims().rearrange(by_tile, g=2, j=4)
    m_dram = feature_m.flatten_outer_dims().rearrange(by_tile, g=2, j=4)
    out_dram = {
        "x": out_0.flatten_outer_dims().rearrange(by_tile, g=2, j=4),
        "m": out_1.flatten_outer_dims().rearrange(by_tile, g=2, j=4),
    }

    with ExitStack() as ctx:
        keep = ctx.enter_context(tc.tile_pool(name="keep", bufs=1))
        stage = ctx.enter_context(tc.tile_pool(name="stage", bufs=2))
        small = ctx.enter_context(tc.tile_pool(name="small", bufs=4))
        psum = ctx.enter_context(tc.psum_pool(name="psum", bufs=8))
        ctx.enter_context(tc.manual_schedule())

        warm = small.tile([P, 2], F32, name="warm")
        nc.vector.memset(warm[:, 0:1], 0.0)
        nc.scalar.activation(out=warm[:, 1:2], in_=warm[:, 0:1], func=ACT.Exp)

        zeros = keep.tile([P, HALF], BF16, name="zeros")
        nc.vector.memset(zeros[:], 0.0)
        ident_f32 = keep.tile([P, P], F32, name="ident_f32")
        make_identity(nc, ident_f32[:])

        x_sb = [keep.tile([P, 4, N], BF16, name="x_sb%d" % g, align_bytes=64) for g in range(2)]
        m_sb = [keep.tile([P, 4, N], BF16, name="m_sb%d" % g, align_bytes=64) for g in range(2)]
        attn_sb = [keep.tile([P, 4, N], BF16, name="attn_sb%d" % g, align_bytes=64) for g in range(2)]

        def load(sb, dram, g, j0, j1, lo=0, hi=N):
            nc.sync.dma_start(out=sb[g][:, j0:j1, lo:hi], in_=dram[:, g, j0:j1, lo:hi])

        load(m_sb, m_dram, 0, 0, 2, 0, HALF)
        load(m_sb, m_dram, 0, 0, 2, HALF, N)
        load(m_sb, m_dram, 0, 2, 4)
        load(m_sb, m_dram, 1, 0, 2)
        load(m_sb, m_dram, 1, 2, 4)
        load(x_sb, x_dram, 0, 0, 1)
        load(x_sb, x_dram, 0, 1, 4)
        load(x_sb, x_dram, 1, 0, 2)
        load(x_sb, x_dram, 1, 2, 4)

        def operand(name, words):
            return (
                keep.tile([P, words], U32, name=name + "_codes", align_bytes=64),
                keep.tile([P, words], U8, name=name + "_scales", align_bytes=64),
            )

        m_t = operand("m_t", 2 * N)
        x_t_first = operand("x_t_first", N)
        attn_d_last = operand("attn_d_last", N)
        by_channel = [operand("chunk%d" % n, HALF) if n not in (3, 4, 5, 6) else None for n in range(8)]
        attn_c = [operand("attn_c%d" % b, HALF) for b in range(4)]
        by_step = {k: operand("step%d" % k, N) for k in range(2, 6)}

        def place_of_x_t(i):
            return (by_step[i - 2], PIECE) if i >= 4 else (x_t_first, PIECE * i)

        def place_of_attn_d(i):
            return (by_step[i + 2], 0) if i < 4 else (attn_d_last, PIECE * (i - 4))

        def place_of_chunk(n):
            return (by_step[n - 1], HALF) if 3 <= n <= 6 else (by_channel[n], 0)

        plain = {"m": m_sb, "x": x_sb, "attn": attn_sb}

        step_grouped = {}

        def group_of_step(k):
            if k not in step_grouped:
                step_grouped[k] = stage.tile([P, 4 * N], BF16, name="step_grouped", bufs=4, align_bytes=64)
            return step_grouped[k]

        def quantise_step(k):
            quantise(by_step[k], 0, step_grouped[k][:])

        def quantise(dst, start, grouped):
            words = slice(start, start + grouped.shape[1] // 4)
            nc.vector.quantize_mx(out=dst[0][:, words].bitcast(FP8X4), scales=dst[1][:, words], in_=grouped)

        def mx_pass(acc, a_place, a_offset, b_place, b_offset, s):
            a, a_start = a_place
            b, b_start = b_place
            a_cols = slice(a_start + a_offset, a_start + a_offset + P)
            b_cols = slice(b_start + b_offset, b_start + b_offset + HALF)
            nc.tensor.matmul_mx(
                out=acc,
                lhsT=a[0][:, a_cols].bitcast(FP8X4),
                lhsT_scale=a[1][:, a_cols],
                rhs=b[0][:, b_cols].bitcast(FP8X4),
                rhs_scale=b[1][:, b_cols],
                start=(s == 0),
                stop=(s == 1),
            )

        def bank(shape, dtype):
            return psum.tile(shape, dtype, name="bank")

        def idle_matmul(bank_tile):
            nc.tensor.matmul(bank_tile, lhsT=zeros[:, 0:P], rhs=zeros[:], start=True, stop=True)

        words_ps = {}
        x_t_grouped = {}
        m_t_grouped = {}

        def transpose_words(key, sb, i):
            words = sb[i // 4][:, i % 4, :].bitcast(F32)
            ps = bank([P, 4, P], F32)
            for n in range(3 if i == 1 else 0):
                idle_matmul(ps[:].rearrange("p b c -> p (b c)"))
            for b in range(4):
                nc.tensor.transpose(ps[:, b, :], words[:, P * b : P * (b + 1)], ident_f32[:])
            words_ps[key, i] = ps[:].rearrange("p (s u) c -> p s c u", s=2, u=2)

        def copy_x_t(i):
            if i >= 4:
                grouped = group_of_step(i - 2)[:, N : 2 * N]
            else:
                x_t_grouped[i] = stage.tile([P, N], BF16, name="x_t_grouped", bufs=4, align_bytes=64)
                grouped = x_t_grouped[i][:]
            nc.scalar.copy(out=grouped.bitcast(F32).rearrange("p (s c u) -> p s c u", s=2, u=2),
                           in_=words_ps["x", i])

        def quantise_x_t(i):
            quantise(x_t_first, PIECE * i, x_t_grouped[i][:])

        def transpose_m_words(g, u, s):
            ps = bank([P, 2, 2, P], F32)
            if s == 0:
                for n in range(4 if (g, u) == (0, 0) else 1):
                    idle_matmul(ps[:].rearrange("p e v c -> p (e v c)"))
            for e in range(2):
                words = m_sb[g][:, 2 * u + e, :].bitcast(F32)
                for v in range(2):
                    b = 2 * s + v
                    nc.tensor.transpose(ps[:, e, v, :], words[:, P * b : P * (b + 1)], ident_f32[:])
            words_ps["m", g, u, s] = ps[:].rearrange("p e v c -> p c e v")

        def copy_m_t(copy, g, u, s):
            m_t_grouped[g, u, s] = stage.tile([P, N], BF16, name="m_t_grouped", bufs=6, align_bytes=64)
            copy(out=m_t_grouped[g, u, s][:].bitcast(F32).rearrange("p (c e v) -> p c e v", e=2, v=2),
                 in_=words_ps["m", g, u, s])

        def quantise_m_t(g, u, s):
            quantise(m_t, s * N + g * HALF + u * PIECE, m_t_grouped[g, u, s][:])

        chunks = [("m", g, h) for g in range(2) for h in range(2)]
        chunks += [("x", g, h) for g in range(2) for h in range(2)]
        chunks += [("attn", g, h) for g in range(2) for h in range(2)]
        chunk_grouped = {}

        def regroup(copy, n, lo, hi):
            name, g, h = chunks[n]
            if n not in chunk_grouped:
                if 3 <= n <= 6:
                    chunk_grouped[n] = group_of_step(n - 1)[:, 2 * N :].rearrange("p (c j) -> p c j", j=4)
                else:
                    chunk_grouped[n] = stage.tile([P, HALF, 4], BF16, name="chunk_grouped", bufs=3, align_bytes=64)
            if name == "attn":
                for c0 in range(lo, hi, P):
                    u, e = divmod(c0 // P, 2)
                    start = h * HALF + u * PIECE
                    pairs = attn_sb[g][:, :, start : start + PIECE].rearrange("p j (c e) -> p e c j", e=2)
                    if e == 0 and hi - c0 >= PIECE:
                        copy(out=chunk_grouped[n][:, c0 : c0 + PIECE, :].rearrange("p (e c) j -> p e c j", e=2), in_=pairs)
                    elif e == 0 or c0 == lo:
                        copy(out=chunk_grouped[n][:, c0 : c0 + P, :], in_=pairs[:, e, :, :])
                return
            copy(out=chunk_grouped[n][:, lo:hi, :].rearrange("p (c i) j -> p c j i", i=4),
                 in_=plain[name][g][:, :, h * HALF + lo : h * HALF + hi].rearrange("p j (c i) -> p c j i", i=4))

        def quantise_chunk(n, lo=0, hi=HALF):
            name, g, h = chunks[n]
            quantise(by_channel[n], lo,
                     chunk_grouped[n][:, lo:hi, :].rearrange("p c j -> p (c j)"))

        logits_ps = {}
        half_max = {}
        shift = {}
        exp_sb = {}
        half_sum = {}
        row_sum = {}
        inv_sum = {}

        def logits(i):
            logits_ps[i] = [bank([P, HALF], F32) for h in range(2)]
            for h in range(2):
                for s in range(2):
                    mx_pass(logits_ps[i][h][:], place_of_x_t(i), s * P, (m_t, s * N + h * HALF), 0, s)

        def row_max(i):
            half_max[i] = small.tile([P, 2], F32, name="half_max")
            for h in range(2):
                nc.vector.tensor_reduce(out=half_max[i][:, h : h + 1], in_=logits_ps[i][h][:], axis=AX.X, op=ALU.max)

        def row_shift(i):
            shift[i] = small.tile([P, 1], F32, name="shift")
            nc.vector.tensor_scalar(out=shift[i][:], in0=half_max[i][:, 0:1], scalar1=half_max[i][:, 1:2],
                                    scalar2=-1.0 / N, op0=ALU.max, op1=ALU.mult)

        def exponentials(i):
            exp_sb[i] = stage.tile([P, N], F32, name="exp_sb", bufs=3)
            half_sum[i] = small.tile([P, 2], F32, name="half_sum")
            for h in range(2):
                nc.scalar.activation(out=exp_sb[i][:, h * HALF : (h + 1) * HALF], in_=logits_ps[i][h][:], func=ACT.Exp,
                                     bias=shift[i][:], scale=1.0 / N, accum_out=half_sum[i][:, h : h + 1])

        def row_total(i):
            row_sum[i] = small.tile([P, 1], F32, name="row_sum")
            nc.vector.tensor_scalar(out=row_sum[i][:], in0=half_sum[i][:, 0:1], scalar1=half_sum[i][:, 1:2],
                                    scalar2=None, op0=ALU.add)

        def reciprocal(i):
            inv_sum[i] = small.tile([P, 1], F32, name="inv_sum")
            nc.vector.reciprocal(out=inv_sum[i][:], in_=row_sum[i][:])

        attn_t_ps = {}
        attn_d_grouped = {}

        def transpose_attn(i):
            words = attn_sb[i // 4][:, i % 4, :].bitcast(F32)
            ps = bank([P, 4, P], F32)
            for n in range(4 if i in (0, 6) else 1):
                idle_matmul(ps[:].rearrange("p b c -> p (b c)"))
            for b in range(4):
                nc.tensor.transpose(ps[:, b, :], words[:, P * b : P * (b + 1)], ident_f32[:])
            attn_t_ps[i] = ps[:].rearrange("p (s u) c -> p s c u", s=2, u=2)

        def copy_attn_d(i):
            if i < 4:
                grouped = group_of_step(i + 2)[:, 0:N]
            else:
                attn_d_grouped[i] = stage.tile([P, N], BF16, name="attn_d_grouped", bufs=3, align_bytes=64)
                grouped = attn_d_grouped[i][:]
            nc.scalar.copy(out=grouped.bitcast(F32).rearrange("p (s c u) -> p s c u", s=2, u=2),
                           in_=attn_t_ps[i])

        def quantise_attn_d(i):
            quantise(attn_d_last, PIECE * (i - 4), attn_d_grouped[i][:])

        acc_ps = {}
        result = {}

        def product(name, i, passes=(0, 1)):
            for h in range(2):
                if passes[0] == 0:
                    acc_ps[name, i, h] = bank([P, HALF], F32)
                for s in passes:
                    if name == "m":
                        mx_pass(acc_ps[name, i, h][:], place_of_attn_d(i), s * P, place_of_chunk(2 * s + h), 0, s)
                    else:
                        mx_pass(acc_ps[name, i, h][:], (attn_c[i // 2], PIECE * s), i % 2 * P, place_of_chunk(4 + 2 * s + h), 0, s)

        def add_residual(name, i, h):
            if h == 0:
                result[name, i] = stage.tile([P, N], F32, name="result", bufs=8)
            cols = slice(h * HALF, (h + 1) * HALF)
            out = result[name, i][:, cols]
            residual = plain[name][i // 4][:, i % 4, cols]
            nc.vector.tensor_tensor(out=out, in0=acc_ps[name, i, h][:], in1=residual, op=ALU.add)

        def store(name, i, lo=0, hi=N):
            nc.sync.dma_start(out=out_dram[name][:, i // 4, i % 4, lo:hi], in_=result[name, i][:, lo:hi])

        V, S = nc.vector.tensor_copy, nc.scalar.copy

        def normalise(k):
            reciprocal(k)
            nc.gpsimd.tensor_scalar(out=attn_sb[k // 4][:, k % 4, :], in0=exp_sb[k][:], scalar1=inv_sum[k][:],
                                    scalar2=0.0, op0=ALU.mult, op1=ALU.add)

        for q in range(4):
            g, u = divmod(q, 2)
            for s in range(2):
                transpose_m_words(g, u, s)
            for s in range(2):
                copy_m_t(nc.vector.tensor_copy if s == 1 and q in (0, 3) else nc.scalar.copy, g, u, s)
            for s in range(2):
                quantise_m_t(g, u, s)
            if q in (1, 2):
                regroup(nc.vector.tensor_copy, 0, PIECE * (q // 2), PIECE * (q // 2 + 1) - (P if q == 2 else 0))
        for i in range(4):
            transpose_words("x", x_sb, i)
            copy_x_t(i)
            if i == 0:
                regroup(nc.scalar.copy, 0, HALF - P, HALF)
            if i < 2:
                quantise_x_t(i)
            if i == 0:
                regroup(nc.vector.tensor_copy, 1, 0, PIECE)
        quantise_chunk(0)
        regroup(nc.scalar.copy, 1, PIECE, HALF)
        logits(0)
        logits(1)
        row_max(0)
        row_shift(0)
        exponentials(0)

        for k in range(TILES - 2):
            late_x = (4 + 2 * k, 5 + 2 * k) if k < 2 else ()
            if k >= 1:
                transpose_attn(k - 1)
            for i in late_x:
                transpose_words("x", x_sb, i)
            if k >= 2:
                quantise_step(k)
                product("m", k - 2)
            else:
                quantise_chunk(k + 1)
                quantise_x_t(k + 2)
            logits(k + 2)
            if k >= 2:
                row_total(k)
            share = (320, 384)[k] if k < 2 else 96
            if share:
                regroup(V, k + 2, 0, share)
            share = (320, 384)[k] if k < 2 else 96
            if share < HALF:
                regroup(S, k + 2, share, HALF)
            if k >= 1:
                copy_attn_d(k - 1)
            for i in late_x:
                copy_x_t(i)
            if k < 2:
                row_total(k)
            normalise(k)
            row_max(k + 1)
            if k >= 2:
                add_residual("m", k - 2, 0)
            row_shift(k + 1)
            exponentials(k + 1)
            if k >= 2:
                add_residual("m", k - 2, 1)
                store("m", k - 2)

        pair_grouped = {}

        def regroup_pair(copy, b, g):
            if b not in pair_grouped:
                pair_grouped[b] = stage.tile([P, 2, PIECE, 4], BF16, name="pair_grouped%d" % (b % 2), bufs=1, align_bytes=64)
            copy(out=pair_grouped[b][:, g, :, :].rearrange("p (e c) j -> p e c j", e=2),
                 in_=attn_sb[g][:, :, PIECE * b : PIECE * (b + 1)].rearrange("p j (c e) -> p e c j", e=2))

        def G(out, in_):
            nc.gpsimd.tensor_scalar(out=out, in0=in_, scalar1=1.0, scalar2=0.0, op0=ALU.mult, op1=ALU.add)

        def quantise_pair(b, parts=(0, 1)):
            first, last = parts[0], parts[-1]
            quantise(attn_c[b], PIECE * first, pair_grouped[b][:, first : last + 1, :, :].rearrange("p g c j -> p (g c j)"))

        def finish(name, i, parts=1):
            for h in range(2):
                add_residual(name, i, h)
                if parts == 2:
                    store(name, i, h * HALF, (h + 1) * HALF)
            if parts == 1:
                store(name, i)

        transpose_attn(5)
        quantise_attn_d(4)
        product("m", 4)
        row_max(7)
        row_shift(7)
        copy_attn_d(5)
        exponentials(7)
        row_total(6)
        normalise(6)
        finish("m", 4)
        transpose_attn(6)
        quantise_attn_d(5)
        product("m", 5)
        regroup_pair(S, 0, 0)
        row_total(7)
        reciprocal(7)
        nc.vector.tensor_scalar(out=attn_sb[1][:, 3, :], in0=exp_sb[7][:], scalar1=inv_sum[7][:], scalar2=None, op0=ALU.mult)
        copy_attn_d(6)
        quantise_chunk(7)
        transpose_attn(7)
        regroup_pair(S, 0, 1)
        quantise_pair(0, (0,))
        quantise_attn_d(6)
        finish("m", 5)
        product("m", 6)
        product("x", 0, (0,))
        quantise_pair(0, (1,))
        regroup_pair(G, 2, 1)
        product("x", 0, (1,))
        copy_attn_d(7)
        regroup_pair(S, 1, 1)
        regroup_pair(S, 1, 0)
        finish("m", 6)
        product("x", 1)
        finish("x", 0)
        quantise_attn_d(7)
        quantise_pair(1)
        regroup_pair(G, 3, 0)
        product("m", 7)
        product("x", 2)
        finish("x", 1)
        regroup_pair(S, 2, 0)
        regroup_pair(S, 3, 1)
        finish("m", 7)
        product("x", 3)
        finish("x", 2)
        quantise_pair(2)
        product("x", 4)
        finish("x", 3, parts=2)
        quantise_pair(3)
        product("x", 5)
        finish("x", 4, parts=2)
        product("x", 6)
        finish("x", 5, parts=2)
        product("x", 7)
        finish("x", 6, parts=2)
        finish("x", 7, parts=2)
